import numpy as np
import ml_dtypes


def mxq(x, axis, fmt="e4m3"):
    dtype, down = {"e4m3": (ml_dtypes.float8_e4m3fn, 7), "e5m2": (ml_dtypes.float8_e5m2, 14)}[fmt]
    v = np.moveaxis(np.asarray(x, np.float32).astype(ml_dtypes.bfloat16).astype(np.float64), axis, -1)
    blocks = v.reshape(v.shape[:-1] + (-1, 32))
    amax = np.abs(blocks).max(-1, keepdims=True)
    byte = np.maximum(np.where(amax > 0, np.frexp(amax)[1] - 1 + 127, 0) - down, 1)
    scale = np.exp2(byte - 127.0)
    codes = (blocks / scale).astype(np.float32).astype(dtype).astype(np.float64)
    return np.moveaxis((codes * scale).reshape(v.shape), -1, axis)


WIDE = False


def mx_kscale(k):
    if not WIDE:
        return np.ones(k)
    levels = np.array([10, -10, 5, -5, 0])
    if k % 512:
        return np.exp2(np.random.permutation(np.resize(levels, k // 32))).repeat(32)
    a = np.empty((k // 512, 16))
    for p in range(k // 512):
        a[p, :8] = np.random.permutation(np.resize(levels, 8))
        for g in range(8):
            far = levels[np.abs(levels - a[p, g]) >= 10]
            a[p, g + 8] = far[np.random.randint(len(far))]
    return np.exp2(a.ravel()).repeat(32)


BF16 = ml_dtypes.bfloat16


def bf(x):
    return np.asarray(x, np.float32).astype(BF16)


def f64(x):
    return np.asarray(x).astype(np.float64)


B, T, C, H, D, L = 1, 4096, 4096, 16, 128, 1024
THETA = 1.0e4


def rope(u, cos, sin):
    u0, u1 = u[..., 0::2], u[..., 1::2]
    c = cos[None, :, None, :]
    s = sin[None, :, None, :]
    o0 = u0 * c - u1 * s
    o1 = u0 * s + u1 * c
    return np.stack([o0, o1], axis=-1).reshape(u.shape)


def setup_inputs():
    s, t = mx_kscale(C), mx_kscale(L)
    inv_freq = 1.0 / (THETA ** (np.arange(0, D, 2) / D))
    ang = np.outer(np.arange(T), inv_freq)
    return {"x": bf(np.random.standard_normal((B, T, C)) * s),
            "freqs_cos": bf(np.cos(ang)),
            "freqs_sin": bf(np.sin(ang)),
            "wq": bf(np.random.standard_normal((H * D, C)) * 2.0 / np.sqrt(C) / s),
            "wkv_down": bf(np.random.standard_normal((L, C)) / np.sqrt(C) / s * t[:, None]),
            "wk_up": bf(np.random.standard_normal((D, L)) / np.sqrt(L) / t),
            "wv_up": bf(np.random.standard_normal((D, L)) / np.sqrt(L) / t)}


def reference(x, freqs_cos, freqs_sin, wq, wkv_down, wk_up, wv_up):
    cos, sin = f64(freqs_cos), f64(freqs_sin)
    xq = mxq(f64(x), 2, "e4m3")
    q = (xq @ mxq(f64(wq), 1, "e4m3").T).reshape(B, T, H, D)
    kv_latent = xq @ mxq(f64(wkv_down), 1, "e4m3").T
    lq = mxq(kv_latent, 2, "e4m3")
    k = lq @ mxq(f64(wk_up), 1, "e4m3").T
    v = lq @ mxq(f64(wv_up), 1, "e4m3").T
    q_rot = rope(q, cos, sin)
    k_rot = rope(k[:, :, None, :], cos, sin)[:, :, 0, :]
    return q_rot, k_rot, v

@@ -1,0 +1,380 @@
+from contextlib import ExitStack
+
+import concourse.mybir as mybir
+from concourse.masks import make_identity
+
+F32 = mybir.dt.float32
+BF16 = mybir.dt.bfloat16
+U32 = mybir.dt.uint32
+U8 = mybir.dt.uint8
+FP8X4 = mybir.dt.float8_e4m3fn_x4
+MULT = mybir.AluOpType.mult
+ADD = mybir.AluOpType.add
+
+P = 128
+T = 4096
+C = 4096
+NQ = 2048
+LAT = 1024
+D = 128
+NPASS = C // 512
+NTILE = T // P
+NBLK = NTILE // 2
+FLOPS = 2 * T * C * (NQ + LAT) + 2 * T * LAT * 2 * D
+
+NXB = 4
+NHEAD = 4
+AHEAD = 4
+LAG = 1
+PER = 3
+PER_HEAD = 1
+
+
+def tile_attention_pa_l_kernel(tc, x, freqs_cos, freqs_sin, wq, wkv_down, wk_up, wv_up, out_0, out_1, out_2):
+    nc = tc.nc
+    with ExitStack() as ctx:
+        const = ctx.enter_context(tc.tile_pool(name="const", bufs=1))
+        xpool = ctx.enter_context(tc.tile_pool(name="xpool", bufs=NXB))
+        rawp = ctx.enter_context(tc.tile_pool(name="rawp", bufs=AHEAD + 1))
+        srtp = ctx.enter_context(tc.tile_pool(name="srtp", bufs=3))
+        grpp = ctx.enter_context(tc.tile_pool(name="grpp", bufs=3))
+        latp = ctx.enter_context(tc.tile_pool(name="latp", bufs=2))
+        latcp = ctx.enter_context(tc.tile_pool(name="latcp", bufs=NHEAD))
+        kvp = ctx.enter_context(tc.tile_pool(name="kvp", bufs=1))
+        ropep = ctx.enter_context(tc.tile_pool(name="ropep", bufs=2))
+        outp = ctx.enter_context(tc.tile_pool(name="outp", bufs=3))
+        pst = ctx.enter_context(tc.psum_pool(name="pst", bufs=4))
+        psa = ctx.enter_context(tc.psum_pool(name="psa", bufs=4))
+        ctx.enter_context(tc.manual_schedule())
+
+        xv = x[0, :, :].rearrange("(p a) k -> p a k", a=NTILE)
+        qv = out_0[0, :, :, :].rearrange("(p a) h d -> p a (h d)", a=NTILE)
+        kv = out_1[0, :, :].rearrange("(p a) d -> p a d", a=NTILE)
+        vv = out_2[0, :, :].rearrange("(p a) d -> p a d", a=NTILE)
+
+        warm = const.tile([P, 8], F32, name="warm")
+        warm2 = const.tile([P, 8], F32, name="warm2")
+        nc.vector.memset(warm[:], 0.0)
+        nc.scalar.copy(out=warm2[:], in_=warm[:])
+        ident = const.tile([P, P], F32, name="ident")
+        make_identity(nc, ident[:])
+        trig = const.tile([P, 3, NTILE, 64], BF16, name="trig")
+
+        def load_trig():
+            nc.gpsimd.dma_start(out=trig[:, 0, :, :], in_=freqs_sin.rearrange("(p a) j -> p a j", a=NTILE))
+            nc.gpsimd.dma_start(out=trig[:, 1, :, :], in_=freqs_cos.rearrange("(p a) j -> p a j", a=NTILE))
+            nc.gpsimd.tensor_scalar(out=trig[:, 2, :, :], in0=trig[:, 0, :, :], scalar1=-1.0, scalar2=0.0, op0=MULT, op1=ADD)
+
+        wqc = [const.tile([P, NPASS, 512], U32, name="wqc%d" % c, align_bytes=64) for c in range(4)]
+        wqs = [const.tile([P, 2, 512], U8, name="wqs%d" % c, align_bytes=64) for c in range(4)]
+        kvc = [const.tile([P, NPASS, 512], U32, name="kvc%d" % g, align_bytes=64) for g in range(2)]
+        kvs = [const.tile([P, 2, 512], U8, name="kvs%d" % g, align_bytes=64) for g in range(2)]
+        upc = const.tile([P, 2, 256], U32, name="upc", align_bytes=64)
+        ups = const.tile([P, 2, 256], U8, name="ups", align_bytes=64)
+        xt = {}
+
+        def plane(tile_s, g, lo, hi):
+            return tile_s[4 * (g % 4):P, g // 4, lo:hi]
+
+        jobs = []
+
+        def add_x(b):
+            for a1 in range(2):
+                for h in range(2):
+                    jobs.append(("x", b, a1, h))
+
+        def add_w(kind, c):
+            for rt in range(4):
+                for h in range(2):
+                    jobs.append((kind, c, rt, h))
+
+        add_x(0)
+        add_w("kv", 0)
+        for b in range(1, NHEAD):
+            add_x(b)
+        add_w("kv", 1)
+        jobs.append(("up", 0, 0, 0))
+        jobs.append(("up", 1, 0, 0))
+        for c in range(4):
+            add_w("wq", c)
+        for b in range(NHEAD, NBLK):
+            add_x(b)
+        jidx = {}
+        for i, j in enumerate(jobs):
+            jidx[j] = i
+
+        first_wq = jidx[("wq", 0, 0, 0)]
+        last_w = jidx[("wq", 3, 3, 1)]
+
+        def job_srcs(j):
+            kind, c, rt, h = j
+            ks = slice(2048 * h, 2048 * (h + 1))
+            if kind == "x":
+                return [(0, P, xv[:, 2 * c + rt, ks])]
+            if kind == "kv":
+                return [(0, P, wkv_down[512 * c + rt:512 * (c + 1):4, ks])]
+            if kind == "wq":
+                base = 512 * c + 256 * (rt % 2) + rt // 2
+                return [(0, P, wq[base:base + 255:2, ks])]
+            if c == 0:
+                return [(0, 64, wk_up[0:D:2, :]), (64, P, wk_up[1:D:2, :])]
+            return [(0, P, wv_up[:, :])]
+
+        def job_dst(j, g):
+            kind, c, rt, h = j
+            lo, hi = P * rt, P * (rt + 1)
+            if kind == "x":
+                return xt[c][0][:, g, lo:hi], plane(xt[c][1], g, lo, hi)
+            if kind == "kv":
+                return kvc[c][:, g, lo:hi], plane(kvs[c], g, lo, hi)
+            if kind == "wq":
+                return wqc[c][:, g, lo:hi], plane(wqs[c], g, lo, hi)
+            return upc[:, g, P * c:P * (c + 1)], ups[:, g, P * c:P * (c + 1)]
+
+        state = {}
+
+        def width(j):
+            return 1024 if j[0] == "up" else 2048
+
+        def load(i):
+            j = jobs[i]
+            w = width(j)
+            raw = rawp.tile([P, 2048], BF16, name="raw")
+            for lo, hi, src in job_srcs(j):
+                nc.sync.dma_start(out=raw[lo:hi, 0:w], in_=src)
+            state[i] = {"raw": raw}
+
+        def sort(i):
+            w = width(jobs[i]) // 2
+            srt = srtp.tile([P, 1024], F32, name="srt")
+            words = state[i]["raw"][:, 0:2 * w].bitcast(F32)
+            if jobs[i][0] == "up":
+                nc.vector.tensor_copy(
+                    out=srt[:].rearrange("r (u g p) -> r g u p", u=2, p=P)[:, 0:2, :, :],
+                    in_=words.rearrange("r (g p u) -> r g u p", u=2, p=P),
+                )
+            else:
+                for u in range(2):
+                    dst = srt[:, 512 * u:512 * (u + 1)].rearrange("r (g m s) -> r g m s", m=16, s=8)
+                    src = words.rearrange("r (g m u s) -> r g u m s", u=2, m=16, s=8)[:, :, u, :, :]
+                    if i < first_wq or (i <= last_w and u == 0):
+                        nc.vector.tensor_copy(out=dst, in_=src)
+                    else:
+                        nc.scalar.copy(out=dst, in_=src)
+            state[i]["srt"] = srt
+
+        def prep(i):
+            j = jobs[i]
+            nbank = width(j) // 1024
+            if j[0] == "x" and j[2] == 0 and j[3] == 0:
+                xc_new = xpool.tile([P, NPASS, 256], U32, name="xc", align_bytes=64)
+                xs_new = xpool.tile([P, 2, 256], U8, name="xs", align_bytes=64)
+                xt[j[1]] = (xc_new, xs_new)
+            srt = state[i]["srt"]
+            banks = []
+            for bk in range(nbank):
+                tb = pst.tile([P, 512], F32, name="tb")
+                for s in range(4):
+                    col = 512 * (s % 2) + P * (2 * bk + s // 2)
+                    nc.tensor.transpose(out=tb[:, P * s:P * (s + 1)], in_=srt[:, col:col + P], identity=ident[:])
+                banks.append(tb)
+            grps = []
+            for bk in range(nbank):
+                grp = grpp.tile([P, 512], F32, name="grp", align_bytes=64)
+                nc.scalar.copy(
+                    out=grp[:].rearrange("p (g r u) -> p g r u", g=2, u=2),
+                    in_=banks[bk][:].rearrange("p (g u r) -> p g r u", g=2, u=2),
+                )
+                grps.append(grp)
+            for bk in range(nbank):
+                for g2 in range(2):
+                    g = 4 * j[3] + 2 * bk + g2
+                    codes, scl = job_dst(j, g)
+                    nc.vector.quantize_mx(out=codes.bitcast(FP8X4), scales=scl, in_=grps[bk][:].bitcast(BF16)[:, 512 * g2:512 * (g2 + 1)])
+            state.pop(i)
+
+        later = []
+
+        def flush():
+            n = len(later)
+            for i in range(n):
+                later.pop(0)()
+
+        def unit_q(b, a1, c):
+            a = 2 * b + a1
+            xc, xs = xt[b]
+            acc = psa.tile([P, 512], F32, name="acc")
+            for g in range(NPASS):
+                nc.tensor.matmul_mx(
+                    out=acc[:],
+                    lhsT=xc[:, g, P * a1:P * (a1 + 1)].bitcast(FP8X4), lhsT_scale=plane(xs, g, P * a1, P * (a1 + 1)),
+                    rhs=wqc[c][:, g, :].bitcast(FP8X4), rhs_scale=plane(wqs[c], g, 0, 512),
+                    start=(g == 0), stop=(g == NPASS - 1),
+                )
+            pr = ropep.tile([P, 2, 2, 256], F32, name="pr")
+            av = acc[:].rearrange("p (e h j) -> p e h j", e=2, h=4)
+            for e1 in range(2):
+                tg = trig[:, 1 - e1:3 - e1, a, :].unsqueeze(2).to_broadcast([P, 2, 4, 64])
+                nc.vector.tensor_tensor(out=pr[:, e1, :, :].rearrange("p e (h j) -> p e h j", h=4), in0=av, in1=tg, op=MULT)
+            oo = ropep.tile([P, 2, 256], F32, name="oo")
+            nc.vector.tensor_tensor(out=oo[:], in0=pr[:, :, 0, :], in1=pr[:, :, 1, :], op=ADD)
+            flush()
+
+            def fin():
+                ost = outp.tile([P, 512], F32, name="ost")
+                nc.scalar.copy(out=ost[:].rearrange("p (m e) -> p m e", e=2), in_=oo[:].rearrange("p e m -> p m e"))
+                nc.gpsimd.dma_start(out=qv[:, a, 512 * c:512 * (c + 1)], in_=ost[:])
+            later.append(fin)
+
+        lat = {}
+
+        def unit_l(b, gg, q):
+            xc, xs = xt[b]
+            acc = psa.tile([P, 512], F32, name="acc")
+            for t2 in range(2):
+                t = 2 * q + t2
+                for g in range(NPASS):
+                    nc.tensor.matmul_mx(
+                        out=acc[:, 256 * t2:256 * (t2 + 1)],
+                        lhsT=kvc[gg][:, g, P * t:P * (t + 1)].bitcast(FP8X4), lhsT_scale=plane(kvs[gg], g, P * t, P * (t + 1)),
+                        rhs=xc[:, g, :].bitcast(FP8X4), rhs_scale=plane(xs, g, 0, 256),
+                        start=(g == 0), stop=(g == NPASS - 1),
+                    )
+            flush()
+            if q == 0:
+                lat4_new = latp.tile([P, 4, 256], BF16, name="lat4")
+                lat[(b, gg)] = lat4_new
+            if q == 0 and gg == 0:
+                latc_new = latcp.tile([P, 2, 256], U32, name="latc", align_bytes=64)
+                lats_new = latcp.tile([P, 2, 256], U8, name="lats", align_bytes=64)
+                lat[b] = (latc_new, lats_new)
+            lat4 = lat[(b, gg)]
+
+            def quant():
+                gl = lat[(b, gg, "gl")]
+                nc.vector.quantize_mx(out=lat[b][0][:, gg, :].bitcast(FP8X4), scales=lat[b][1][:, gg, :], in_=gl[:])
+
+            def weave():
+                gl = latp.tile([P, 1024], BF16, name="gl", align_bytes=64)
+                lat[(b, gg, "gl")] = gl
+                nc.vector.tensor_copy(out=gl[:].rearrange("p (n t) -> p n t", t=4), in_=lat4[:].rearrange("p t n -> p n t"))
+                later.append(quant)
+
+            def out_of_psum():
+                nc.scalar.copy(out=lat4[:, 2 * q:2 * q + 2, :], in_=acc[:].rearrange("p (t n) -> p t n", t=2))
+                if q == 1:
+                    later.append(weave)
+            later.append(out_of_psum)
+
+        def unit_s2(b):
+            while len(later) > 0:
+                flush()
+            latc, lats = lat[b]
+            acc = psa.tile([P, 512], F32, name="acc")
+            for a1 in range(2):
+                for gg in range(2):
+                    nc.tensor.matmul_mx(
+                        out=acc[:, 256 * a1:256 * (a1 + 1)],
+                        lhsT=latc[:, gg, P * a1:P * (a1 + 1)].bitcast(FP8X4), lhsT_scale=lats[:, gg, P * a1:P * (a1 + 1)],
+                        rhs=upc[:, gg, :].bitcast(FP8X4), rhs_scale=ups[:, gg, :],
+                        start=(gg == 0), stop=(gg == 1),
+                    )
+            av = acc[:].rearrange("p (a s e j) -> p a s e j", a=2, s=2, e=2)
+            prk = kvp.tile([P, 2, 2, 2, 64], F32, name="prk")
+            for e1 in range(2):
+                tg = trig[:, 1 - e1:3 - e1, 2 * b:2 * b + 2, :].rearrange("p e a j -> p a e j")
+                nc.vector.tensor_tensor(out=prk[:, e1, :, :, :], in0=av[:, :, 0, :, :], in1=tg, op=MULT)
+            ok = kvp.tile([P, 2, 2, 64], F32, name="ok")
+            nc.vector.tensor_tensor(out=ok[:], in0=prk[:, :, :, 0, :], in1=prk[:, :, :, 1, :], op=ADD)
+            vst = kvp.tile([P, 2, D], F32, name="vst")
+            nc.vector.tensor_copy(out=vst[:], in_=acc[:].rearrange("p (a s d) -> p a s d", a=2, s=2)[:, :, 1, :])
+            nc.gpsimd.dma_start(out=vv[:, 2 * b:2 * b + 2, :], in_=vst[:])
+            flush()
+
+            def fin():
+                kst = kvp.tile([P, 2, D], F32, name="kst")
+                nc.scalar.copy(out=kst[:].rearrange("p a (j e) -> p a j e", e=2), in_=ok[:].rearrange("p e a j -> p a j e"))
+                nc.gpsimd.dma_start(out=kv[:, 2 * b:2 * b + 2, :], in_=kst[:])
+            later.append(fin)
+
+        units = []
+        for gg in range(2):
+            for b in range(NHEAD):
+                units.append(("L", b, gg, 0))
+                units.append(("L", b, gg, 1))
+        for c in range(4):
+            for b in range(NHEAD):
+                units.append(("Q", b, 0, c))
+                units.append(("Q", b, 1, c))
+                if c == 0:
+                    units.append(("S", b, 0, 0))
+        for b in range(NHEAD, NBLK - 1):
+            for s in range(4):
+                units.append(("L", b, s // 2, s % 2))
+                units.append(("Q", b, s // 2, 2 * (s % 2)))
+                units.append(("Q", b, s // 2, 2 * (s % 2) + 1))
+                if s == 0 and b > NHEAD:
+                    units.append(("S", b - 1, 0, 0))
+        b = NBLK - 1
+        for s in range(4):
+            units.append(("L", b, s // 2, s % 2))
+        units.append(("S", b - 1, 0, 0))
+        for s in range(8):
+            units.append(("Q", b, s // 4, s % 4))
+            if s == 3:
+                units.append(("S", b, 0, 0))
+
+        def need(u):
+            kind, b, i1, i2 = u
+            if kind == "Q":
+                return max(jidx[("x", b, i1, 1)], jidx[("wq", i2, 3, 1)])
+            if kind == "L":
+                return max(jidx[("x", b, 1, 1)], jidx[("kv", i1, 2 * i2 + 1, 1)])
+            return jidx[("up", 1, 0, 0)]
+
+        last_unit = {}
+        for i, u in enumerate(units):
+            if u[0] != "S":
+                last_unit[u[1]] = i
+
+        def gate(j):
+            if j[0] == "x" and j[1] >= NXB:
+                return last_unit[j[1] - NXB] + 1
+            return 0
+
+        nj, nu = len(jobs), len(units)
+        for i in range(AHEAD):
+            load(i)
+        sort(0)
+        sort(1)
+        ju, uu = 0, 0
+        while ju < nj or uu < nu:
+            moved = False
+            if ju < nj and gate(jobs[ju]) <= uu:
+                if ju + AHEAD < nj:
+                    load(ju + AHEAD)
+                if ju == 8:
+                    load_trig()
+                if ju + 2 < nj:
+                    sort(ju + 2)
+                prep(ju)
+                flush()
+                ju += 1
+                moved = True
+            n = 0
+            held = ju >= nj or gate(jobs[ju]) > uu
+            per = PER if ju > last_w else PER_HEAD
+            while uu < nu and n < per and need(units[uu]) + (0 if held else LAG) < ju:
+                kind, b, i1, i2 = units[uu]
+                if kind == "Q":
+                    unit_q(b, i1, i2)
+                elif kind == "L":
+                    unit_l(b, i1, i2)
+                else:
+                    unit_s2(b)
+                uu += 1
+                n += 1
+                moved = True
+            assert moved
+        while len(later) > 0:
+            flush()

@@ -22,12 +22,13 @@ NTILE = T // P
 NBLK = NTILE // 2
 FLOPS = 2 * T * C * (NQ + LAT) + 2 * T * LAT * 2 * D
 
-NXB = 4
-NHEAD = 4
-AHEAD = 4
+NXB = 3
+NHEAD = 3
+AHEAD = 2
 LAG = 1
-PER = 3
-PER_HEAD = 1
+SPU = 2
+SPU_HEAD = 4
+NDVE = 3
 
 
 def tile_attention_pa_l_kernel(tc, x, freqs_cos, freqs_sin, wq, wkv_down, wk_up, wv_up, out_0, out_1, out_2):
@@ -36,9 +37,10 @@ def tile_attention_pa_l_kernel(tc, x, freqs_cos, freqs_sin, wq, wkv_down, wk_up,
         const = ctx.enter_context(tc.tile_pool(name="const", bufs=1))
         xpool = ctx.enter_context(tc.tile_pool(name="xpool", bufs=NXB))
         rawp = ctx.enter_context(tc.tile_pool(name="rawp", bufs=AHEAD + 1))
-        srtp = ctx.enter_context(tc.tile_pool(name="srtp", bufs=3))
+        srtp = ctx.enter_context(tc.tile_pool(name="srtp", bufs=2))
+        onep = ctx.enter_context(tc.tile_pool(name="onep", bufs=1))
         grpp = ctx.enter_context(tc.tile_pool(name="grpp", bufs=3))
-        latp = ctx.enter_context(tc.tile_pool(name="latp", bufs=2))
+        latp = ctx.enter_context(tc.tile_pool(name="latp", bufs=NHEAD))
         latcp = ctx.enter_context(tc.tile_pool(name="latcp", bufs=NHEAD))
         kvp = ctx.enter_context(tc.tile_pool(name="kvp", bufs=1))
         ropep = ctx.enter_context(tc.tile_pool(name="ropep", bufs=2))
@@ -80,48 +82,53 @@ def tile_attention_pa_l_kernel(tc, x, freqs_cos, freqs_sin, wq, wkv_down, wk_up,
 
         def add_x(b):
             for a1 in range(2):
-                for h in range(2):
-                    jobs.append(("x", b, a1, h))
+                jobs.append(("x", b, a1))
 
         def add_w(kind, c):
             for rt in range(4):
-                for h in range(2):
-                    jobs.append((kind, c, rt, h))
+                jobs.append((kind, c, rt))
 
         add_x(0)
         add_w("kv", 0)
         for b in range(1, NHEAD):
             add_x(b)
-        add_w("kv", 1)
-        jobs.append(("up", 0, 0, 0))
-        jobs.append(("up", 1, 0, 0))
-        for c in range(4):
+        for rt in range(4):
+            jobs.append(("wq", 0, rt))
+            jobs.append(("kv", 1, rt))
+        jobs.append(("up", 0, 0))
+        jobs.append(("up", 1, 0))
+        for c in range(1, 4):
             add_w("wq", c)
         for b in range(NHEAD, NBLK):
             add_x(b)
+        nj = len(jobs)
         jidx = {}
         for i, j in enumerate(jobs):
             jidx[j] = i
 
-        first_wq = jidx[("wq", 0, 0, 0)]
-        last_w = jidx[("wq", 3, 3, 1)]
+        first_wq = jidx[("wq", 0, 0)]
+        last_w = jidx[("wq", 3, 3)]
+
+        def on_dve(j):
+            return j[0] == "x" and j[1] >= NDVE
 
         def job_srcs(j):
-            kind, c, rt, h = j
-            ks = slice(2048 * h, 2048 * (h + 1))
+            kind, c, rt = j
+            if on_dve(j):
+                return [(32 * i, 32 * (i + 1), xv[:, 2 * c + rt, 1024 * i:1024 * (i + 1)].rearrange("(j b) k -> b j k", j=4)) for i in range(4)]
             if kind == "x":
-                return [(0, P, xv[:, 2 * c + rt, ks])]
+                return [(0, P, xv[:, 2 * c + rt, :])]
             if kind == "kv":
-                return [(0, P, wkv_down[512 * c + rt:512 * (c + 1):4, ks])]
+                return [(0, P, wkv_down[512 * c + rt:512 * (c + 1):4, :])]
             if kind == "wq":
                 base = 512 * c + 256 * (rt % 2) + rt // 2
-                return [(0, P, wq[base:base + 255:2, ks])]
+                return [(0, P, wq[base:base + 255:2, :])]
             if c == 0:
                 return [(0, 64, wk_up[0:D:2, :]), (64, P, wk_up[1:D:2, :])]
             return [(0, P, wv_up[:, :])]
 
         def job_dst(j, g):
-            kind, c, rt, h = j
+            kind, c, rt = j
             lo, hi = P * rt, P * (rt + 1)
             if kind == "x":
                 return xt[c][0][:, g, lo:hi], plane(xt[c][1], g, lo, hi)
@@ -134,64 +141,110 @@ def tile_attention_pa_l_kernel(tc, x, freqs_cos, freqs_sin, wq, wkv_down, wk_up,
         state = {}
 
         def width(j):
-            return 1024 if j[0] == "up" else 2048
+            return 1024 if j[0] == "up" else 4096
 
         def load(i):
             j = jobs[i]
             w = width(j)
-            raw = rawp.tile([P, 2048], BF16, name="raw")
+            raw = rawp.tile([P, 4096], BF16, name="raw")
             for lo, hi, src in job_srcs(j):
-                nc.sync.dma_start(out=raw[lo:hi, 0:w], in_=src)
+                if on_dve(j):
+                    nc.sync.dma_start(out=raw[lo:hi, :].rearrange("b (j k) -> b j k", j=4), in_=src)
+                else:
+                    nc.sync.dma_start(out=raw[lo:hi, 0:w], in_=src)
             state[i] = {"raw": raw}
 
-        def sort(i):
+        def sort(i, half):
             w = width(jobs[i]) // 2
-            srt = srtp.tile([P, 1024], F32, name="srt")
+            if half == 0:
+                srt_new = srtp.tile([P, 2048], F32, name="srt", align_bytes=64)
+                state[i]["srt"] = srt_new
+            srt = state[i]["srt"]
             words = state[i]["raw"][:, 0:2 * w].bitcast(F32)
+            if jobs[i][0] == "up" and half == 1:
+                return
             if jobs[i][0] == "up":
                 nc.vector.tensor_copy(
                     out=srt[:].rearrange("r (u g p) -> r g u p", u=2, p=P)[:, 0:2, :, :],
                     in_=words.rearrange("r (g p u) -> r g u p", u=2, p=P),
                 )
             else:
-                for u in range(2):
-                    dst = srt[:, 512 * u:512 * (u + 1)].rearrange("r (g m s) -> r g m s", m=16, s=8)
-                    src = words.rearrange("r (g m u s) -> r g u m s", u=2, m=16, s=8)[:, :, u, :, :]
+                for u in range(half, half + 1):
+                    dst = srt[:, 1024 * u:1024 * (u + 1)].rearrange("r (g m s) -> r g m s", m=16, s=8)
+                    src = words.rearrange("r (m g u s) -> r u g m s", g=8, u=2, s=8)[:, u, :, :, :]
                     if i < first_wq or (i <= last_w and u == 0):
                         nc.vector.tensor_copy(out=dst, in_=src)
                     else:
                         nc.scalar.copy(out=dst, in_=src)
-            state[i]["srt"] = srt
 
-        def prep(i):
+        def job_steps(i):
             j = jobs[i]
             nbank = width(j) // 1024
-            if j[0] == "x" and j[2] == 0 and j[3] == 0:
-                xc_new = xpool.tile([P, NPASS, 256], U32, name="xc", align_bytes=64)
-                xs_new = xpool.tile([P, 2, 256], U8, name="xs", align_bytes=64)
-                xt[j[1]] = (xc_new, xs_new)
-            srt = state[i]["srt"]
-            banks = []
-            for bk in range(nbank):
-                tb = pst.tile([P, 512], F32, name="tb")
-                for s in range(4):
-                    col = 512 * (s % 2) + P * (2 * bk + s // 2)
-                    nc.tensor.transpose(out=tb[:, P * s:P * (s + 1)], in_=srt[:, col:col + P], identity=ident[:])
-                banks.append(tb)
-            grps = []
-            for bk in range(nbank):
+            st = state[i]
+            turned = []
+            grps = {}
+            out = []
+
+            def begin():
+                if i + AHEAD < nj:
+                    load(i + AHEAD)
+                if i == 4:
+                    load_trig()
+                if j[0] == "x" and j[2] == 0:
+                    xc_new = xpool.tile([P, NPASS, 256], U32, name="xc", align_bytes=64)
+                    xs_new = xpool.tile([P, 2, 256], U8, name="xs", align_bytes=64)
+                    xt[j[1]] = (xc_new, xs_new)
+                srt = st["srt"]
+                if on_dve(j):
+                    tr = onep.tile([P, 2048], F32, name="tr", align_bytes=64)
+                    st["tr"] = tr
+                    nc.vector.transpose(out=tr[:, 0:1024], in_=srt[:, 0:1024])
+                    for bk in range(nbank):
+                        turned.append(tr[:].rearrange("p (u g r) -> p g r u", u=2, g=8)[:, 2 * bk:2 * bk + 2, :, :])
+                else:
+                    for bk in range(nbank):
+                        tb = pst.tile([P, 512], F32, name="tb")
+                        for s in range(4):
+                            col = 1024 * (s % 2) + P * (2 * bk + s // 2)
+                            nc.tensor.transpose(out=tb[:, P * s:P * (s + 1)], in_=srt[:, col:col + P], identity=ident[:])
+                        turned.append(tb[:].rearrange("p (g u r) -> p g r u", g=2, u=2))
+
+            def second_half():
+                nc.vector.transpose(out=st["tr"][:, 1024:2048], in_=st["srt"][:, 1024:2048])
+
+            def weave_bank(bk):
                 grp = grpp.tile([P, 512], F32, name="grp", align_bytes=64)
-                nc.scalar.copy(
-                    out=grp[:].rearrange("p (g r u) -> p g r u", g=2, u=2),
-                    in_=banks[bk][:].rearrange("p (g u r) -> p g r u", g=2, u=2),
-                )
-                grps.append(grp)
-            for bk in range(nbank):
+                nc.scalar.copy(out=grp[:].rearrange("p (g r u) -> p g r u", g=2, u=2), in_=turned[bk])
+                grps[bk] = grp
+
+            def quant_bank(bk):
                 for g2 in range(2):
-                    g = 4 * j[3] + 2 * bk + g2
+                    g = 2 * bk + g2
                     codes, scl = job_dst(j, g)
                     nc.vector.quantize_mx(out=codes.bitcast(FP8X4), scales=scl, in_=grps[bk][:].bitcast(BF16)[:, 512 * g2:512 * (g2 + 1)])
-            state.pop(i)
+
+            def sort_next(half):
+                def run():
+                    sort(i + 1, half)
+                return run
+
+            def bank_step(bk):
+                def run():
+                    if bk + 1 < nbank:
+                        weave_bank(bk + 1)
+                    if bk >= 0:
+                        quant_bank(bk)
+                return run
+
+            out.append(begin)
+            if on_dve(j):
+                out.append(second_half)
+            if i + 1 < nj:
+                out.append(sort_next(0))
+                out.append(sort_next(1))
+            for bk in range(-1, nbank):
+                out.append(bank_step(bk))
+            return out
 
         later = []
 
@@ -211,7 +264,7 @@ def tile_attention_pa_l_kernel(tc, x, freqs_cos, freqs_sin, wq, wkv_down, wk_up,
                     rhs=wqc[c][:, g, :].bitcast(FP8X4), rhs_scale=plane(wqs[c], g, 0, 512),
                     start=(g == 0), stop=(g == NPASS - 1),
                 )
-            pr = ropep.tile([P, 2, 2, 256], F32, name="pr")
+            pr = onep.tile([P, 2, 2, 256], F32, name="pr")
             av = acc[:].rearrange("p (e h j) -> p e h j", e=2, h=4)
             for e1 in range(2):
                 tg = trig[:, 1 - e1:3 - e1, a, :].unsqueeze(2).to_broadcast([P, 2, 4, 64])
@@ -223,7 +276,7 @@ def tile_attention_pa_l_kernel(tc, x, freqs_cos, freqs_sin, wq, wkv_down, wk_up,
             def fin():
                 ost = outp.tile([P, 512], F32, name="ost")
                 nc.scalar.copy(out=ost[:].rearrange("p (m e) -> p m e", e=2), in_=oo[:].rearrange("p e m -> p m e"))
-                nc.gpsimd.dma_start(out=qv[:, a, 512 * c:512 * (c + 1)], in_=ost[:])
+                nc.sync.dma_start(out=qv[:, a, 512 * c:512 * (c + 1)], in_=ost[:])
             later.append(fin)
 
         lat = {}
@@ -255,9 +308,12 @@ def tile_attention_pa_l_kernel(tc, x, freqs_cos, freqs_sin, wq, wkv_down, wk_up,
                 nc.vector.quantize_mx(out=lat[b][0][:, gg, :].bitcast(FP8X4), scales=lat[b][1][:, gg, :], in_=gl[:])
 
             def weave():
-                gl = latp.tile([P, 1024], BF16, name="gl", align_bytes=64)
+                gl = onep.tile([P, 1024], BF16, name="gl", align_bytes=64)
                 lat[(b, gg, "gl")] = gl
-                nc.vector.tensor_copy(out=gl[:].rearrange("p (n t) -> p n t", t=4), in_=lat4[:].rearrange("p t n -> p n t"))
+                if b < NHEAD:
+                    nc.vector.tensor_copy(out=gl[:].rearrange("p (n t) -> p n t", t=4), in_=lat4[:].rearrange("p t n -> p n t"))
+                else:
+                    nc.scalar.copy(out=gl[:].rearrange("p (n t) -> p n t", t=4), in_=lat4[:].rearrange("p t n -> p n t"))
                 later.append(quant)
 
             def out_of_psum():
@@ -288,14 +344,22 @@ def tile_attention_pa_l_kernel(tc, x, freqs_cos, freqs_sin, wq, wkv_down, wk_up,
             nc.vector.tensor_tensor(out=ok[:], in0=prk[:, :, :, 0, :], in1=prk[:, :, :, 1, :], op=ADD)
             vst = kvp.tile([P, 2, D], F32, name="vst")
             nc.vector.tensor_copy(out=vst[:], in_=acc[:].rearrange("p (a s d) -> p a s d", a=2, s=2)[:, :, 1, :])
-            nc.gpsimd.dma_start(out=vv[:, 2 * b:2 * b + 2, :], in_=vst[:])
             flush()
 
             def fin():
                 kst = kvp.tile([P, 2, D], F32, name="kst")
                 nc.scalar.copy(out=kst[:].rearrange("p a (j e) -> p a j e", e=2), in_=ok[:].rearrange("p e a j -> p a j e"))
-                nc.gpsimd.dma_start(out=kv[:, 2 * b:2 * b + 2, :], in_=kst[:])
+                nc.sync.dma_start(out=kv[:, 2 * b:2 * b + 2, :], in_=kst[:])
+                nc.sync.dma_start(out=vv[:, 2 * b:2 * b + 2, :], in_=vst[:])
             later.append(fin)
+
+        def need(u):
+            kind, b, i1, i2 = u
+            if kind == "Q":
+                return max(jidx[("x", b, i1)], jidx[("wq", i2, 3)])
+            if kind == "L":
+                return max(jidx[("x", b, 1)], jidx[("kv", i1, 2 * i2 + 1)])
+            return jidx[("up", 1, 0)]
 
         units = []
         for gg in range(2):
@@ -306,14 +370,22 @@ def tile_attention_pa_l_kernel(tc, x, freqs_cos, freqs_sin, wq, wkv_down, wk_up,
             for b in range(NHEAD):
                 units.append(("Q", b, 0, c))
                 units.append(("Q", b, 1, c))
-                if c == 0:
-                    units.append(("S", b, 0, 0))
-        for b in range(NHEAD, NBLK - 1):
+        units.sort(key=need)
+        at = units.index(("Q", 0, 0, 1))
+        for b in range(NHEAD):
+            units.insert(at + 3 * b + 2, ("S", b, 0, 0))
+        for c in range(4):
+            units.append(("Q", NHEAD, 0, c))
+        for s in range(4):
+            units.append(("L", NHEAD, s // 2, s % 2))
+        for c in range(4):
+            units.append(("Q", NHEAD, 1, c))
+        for b in range(NHEAD + 1, NBLK - 1):
             for s in range(4):
                 units.append(("L", b, s // 2, s % 2))
                 units.append(("Q", b, s // 2, 2 * (s % 2)))
                 units.append(("Q", b, s // 2, 2 * (s % 2) + 1))
-                if s == 0 and b > NHEAD:
+                if s == 0:
                     units.append(("S", b - 1, 0, 0))
         b = NBLK - 1
         for s in range(4):
@@ -324,13 +396,6 @@ def tile_attention_pa_l_kernel(tc, x, freqs_cos, freqs_sin, wq, wkv_down, wk_up,
             if s == 3:
                 units.append(("S", b, 0, 0))
 
-        def need(u):
-            kind, b, i1, i2 = u
-            if kind == "Q":
-                return max(jidx[("x", b, i1, 1)], jidx[("wq", i2, 3, 1)])
-            if kind == "L":
-                return max(jidx[("x", b, 1, 1)], jidx[("kv", i1, 2 * i2 + 1, 1)])
-            return jidx[("up", 1, 0, 0)]
 
         last_unit = {}
         for i, u in enumerate(units):
@@ -342,29 +407,21 @@ def tile_attention_pa_l_kernel(tc, x, freqs_cos, freqs_sin, wq, wkv_down, wk_up,
                 return last_unit[j[1] - NXB] + 1
             return 0
 
-        nj, nu = len(jobs), len(units)
+        nu = len(units)
         for i in range(AHEAD):
             load(i)
-        sort(0)
-        sort(1)
-        ju, uu = 0, 0
-        while ju < nj or uu < nu:
+        sort(0, 0)
+        sort(0, 1)
+        steps = []
+        js, uu = 0, 0
+        while js < nj or uu < nu or len(steps) > 0:
             moved = False
-            if ju < nj and gate(jobs[ju]) <= uu:
-                if ju + AHEAD < nj:
-                    load(ju + AHEAD)
-                if ju == 8:
-                    load_trig()
-                if ju + 2 < nj:
-                    sort(ju + 2)
-                prep(ju)
-                flush()
-                ju += 1
-                moved = True
-            n = 0
-            held = ju >= nj or gate(jobs[ju]) > uu
-            per = PER if ju > last_w else PER_HEAD
-            while uu < nu and n < per and need(units[uu]) + (0 if held else LAG) < ju:
+            if len(steps) == 0 and js < nj and gate(jobs[js]) <= uu:
+                steps.extend(job_steps(js))
+                js += 1
+            done = js if len(steps) == 0 else js - 1
+            held = len(steps) == 0
+            if uu < nu and need(units[uu]) + (0 if held else LAG) < done:
                 kind, b, i1, i2 = units[uu]
                 if kind == "Q":
                     unit_q(b, i1, i2)
@@ -373,8 +430,14 @@ def tile_attention_pa_l_kernel(tc, x, freqs_cos, freqs_sin, wq, wkv_down, wk_up,
                 else:
                     unit_s2(b)
                 uu += 1
-                n += 1
                 moved = True
-            assert moved
+            n = SPU if js > last_w + 3 else SPU_HEAD
+            while n > 0 and len(steps) > 0:
+                steps.pop(0)()
+                n -= 1
+                moved = True
+            if not moved:
+                flush()
+            assert moved or len(later) > 0 or uu < nu
         while len(later) > 0:
             flush()

@@ -65,7 +65,7 @@ def tile_attention_pa_l_kernel(tc, x, freqs_cos, freqs_sin, wq, wkv_down, wk_up,
         def load_trig():
             nc.gpsimd.dma_start(out=trig[:, 0, :, :], in_=freqs_sin.rearrange("(p a) j -> p a j", a=NTILE))
             nc.gpsimd.dma_start(out=trig[:, 1, :, :], in_=freqs_cos.rearrange("(p a) j -> p a j", a=NTILE))
-            nc.gpsimd.tensor_scalar(out=trig[:, 2, :, :], in0=trig[:, 0, :, :], scalar1=-1.0, scalar2=0.0, op0=MULT, op1=ADD)
+            nc.vector.tensor_scalar(out=trig[:, 2, :, :], in0=trig[:, 0, :, :], scalar1=-1.0, scalar2=0.0, op0=MULT, op1=ADD)
 
         wqc = [const.tile([P, NPASS, 512], U32, name="wqc%d" % c, align_bytes=64) for c in range(4)]
         wqs = [const.tile([P, 2, 512], U8, name="wqs%d" % c, align_bytes=64) for c in range(4)]
@@ -172,7 +172,7 @@ def tile_attention_pa_l_kernel(tc, x, freqs_cos, freqs_sin, wq, wkv_down, wk_up,
                 for u in range(half, half + 1):
                     dst = srt[:, 1024 * u:1024 * (u + 1)].rearrange("r (g m s) -> r g m s", m=16, s=8)
                     src = words.rearrange("r (m g u s) -> r u g m s", g=8, u=2, s=8)[:, u, :, :, :]
-                    if i < first_wq or (i <= last_w and u == 0):
+                    if i <= last_w:
                         nc.vector.tensor_copy(out=dst, in_=src)
                     else:
                         nc.scalar.copy(out=dst, in_=src)
@@ -264,18 +264,19 @@ def tile_attention_pa_l_kernel(tc, x, freqs_cos, freqs_sin, wq, wkv_down, wk_up,
                     rhs=wqc[c][:, g, :].bitcast(FP8X4), rhs_scale=plane(wqs[c], g, 0, 512),
                     start=(g == 0), stop=(g == NPASS - 1),
                 )
-            pr = onep.tile([P, 2, 2, 256], F32, name="pr")
+            pr = ropep.tile([P, 2, 2, 256], F32, name="pr")
             av = acc[:].rearrange("p (e h j) -> p e h j", e=2, h=4)
             for e1 in range(2):
                 tg = trig[:, 1 - e1:3 - e1, a, :].unsqueeze(2).to_broadcast([P, 2, 4, 64])
                 nc.vector.tensor_tensor(out=pr[:, e1, :, :].rearrange("p e (h j) -> p e h j", h=4), in0=av, in1=tg, op=MULT)
-            oo = ropep.tile([P, 2, 256], F32, name="oo")
-            nc.vector.tensor_tensor(out=oo[:], in0=pr[:, :, 0, :], in1=pr[:, :, 1, :], op=ADD)
             flush()
 
             def fin():
                 ost = outp.tile([P, 512], F32, name="ost")
-                nc.scalar.copy(out=ost[:].rearrange("p (m e) -> p m e", e=2), in_=oo[:].rearrange("p e m -> p m e"))
+                nc.gpsimd.tensor_tensor(
+                    out=ost[:].rearrange("p (m e) -> p m e", e=2),
+                    in0=pr[:, :, 0, :].rearrange("p e m -> p m e"), in1=pr[:, :, 1, :].rearrange("p e m -> p m e"), op=ADD,
+                )
                 nc.sync.dma_start(out=qv[:, a, 512 * c:512 * (c + 1)], in_=ost[:])
             later.append(fin)
 

@@ -149,7 +149,8 @@ def tile_attention_pa_l_kernel(tc, x, freqs_cos, freqs_sin, wq, wkv_down, wk_up,
             raw = rawp.tile([P, 4096], BF16, name="raw")
             for lo, hi, src in job_srcs(j):
                 if on_dve(j):
-                    nc.sync.dma_start(out=raw[lo:hi, :].rearrange("b (j k) -> b j k", j=4), in_=src)
+                    queue = nc.scalar if lo < 64 else nc.gpsimd
+                    queue.dma_start(out=raw[lo:hi, :].rearrange("b (j k) -> b j k", j=4), in_=src)
                 else:
                     nc.sync.dma_start(out=raw[lo:hi, 0:w], in_=src)
             state[i] = {"raw": raw}

@@ -12,47 +12,46 @@ MULT = mybir.AluOpType.mult
 ADD = mybir.AluOpType.add
 
 P = 128
-T = 4096
-C = 4096
-NQ = 2048
-LAT = 1024
-D = 128
-NPASS = C // 512
-NTILE = T // P
-NBLK = NTILE // 2
-FLOPS = 2 * T * C * (NQ + LAT) + 2 * T * LAT * 2 * D
+TOKENS = 4096
+K1 = 4096
+Q_CHANNELS = 2048
+LATENT = 1024
+HEAD = 128
+PASSES = K1 // 512
+TILES = TOKENS // P
+BLOCKS = TILES // 2
+FLOPS = 2 * TOKENS * K1 * (Q_CHANNELS + LATENT) + 2 * TOKENS * LATENT * 2 * HEAD
 
-NXB = 3
-NHEAD = 3
-AHEAD = 2
-LAG = 1
-SPU = 2
-SPU_HEAD = 4
-NDVE = 3
+X_BUFFERS = 3
+HEAD_BLOCKS = 3
+LOADS_AHEAD = 2
+JOB_LAG = 1
+TRIG_JOB = 12
+STEPS_PER_UNIT = 2
+STEPS_PER_UNIT_HEAD = 5
 
 
 def tile_attention_pa_l_kernel(tc, x, freqs_cos, freqs_sin, wq, wkv_down, wk_up, wv_up, out_0, out_1, out_2):
     nc = tc.nc
     with ExitStack() as ctx:
         const = ctx.enter_context(tc.tile_pool(name="const", bufs=1))
-        xpool = ctx.enter_context(tc.tile_pool(name="xpool", bufs=NXB))
-        rawp = ctx.enter_context(tc.tile_pool(name="rawp", bufs=AHEAD + 1))
+        xpool = ctx.enter_context(tc.tile_pool(name="xpool", bufs=X_BUFFERS))
+        rawp = ctx.enter_context(tc.tile_pool(name="rawp", bufs=LOADS_AHEAD + 1))
         srtp = ctx.enter_context(tc.tile_pool(name="srtp", bufs=2))
         onep = ctx.enter_context(tc.tile_pool(name="onep", bufs=1))
-        grpp = ctx.enter_context(tc.tile_pool(name="grpp", bufs=3))
-        latp = ctx.enter_context(tc.tile_pool(name="latp", bufs=NHEAD))
-        latcp = ctx.enter_context(tc.tile_pool(name="latcp", bufs=NHEAD))
+        grpp = ctx.enter_context(tc.tile_pool(name="grpp", bufs=4))
+        latp = ctx.enter_context(tc.tile_pool(name="latp", bufs=HEAD_BLOCKS))
+        latcp = ctx.enter_context(tc.tile_pool(name="latcp", bufs=HEAD_BLOCKS))
         kvp = ctx.enter_context(tc.tile_pool(name="kvp", bufs=1))
         ropep = ctx.enter_context(tc.tile_pool(name="ropep", bufs=2))
-        outp = ctx.enter_context(tc.tile_pool(name="outp", bufs=3))
-        pst = ctx.enter_context(tc.psum_pool(name="pst", bufs=4))
-        psa = ctx.enter_context(tc.psum_pool(name="psa", bufs=4))
+        outp = ctx.enter_context(tc.tile_pool(name="outp", bufs=4))
+        psa = ctx.enter_context(tc.psum_pool(name="psa", bufs=8))
         ctx.enter_context(tc.manual_schedule())
 
-        xv = x[0, :, :].rearrange("(p a) k -> p a k", a=NTILE)
-        qv = out_0[0, :, :, :].rearrange("(p a) h d -> p a (h d)", a=NTILE)
-        kv = out_1[0, :, :].rearrange("(p a) d -> p a d", a=NTILE)
-        vv = out_2[0, :, :].rearrange("(p a) d -> p a d", a=NTILE)
+        x_view = x[0, :, :].rearrange("(p a) k -> p a k", a=TILES)
+        q_view = out_0[0, :, :, :].rearrange("(p a) h d -> p a (h d)", a=TILES)
+        k_view = out_1[0, :, :].rearrange("(p a) d -> p a d", a=TILES)
+        v_view = out_2[0, :, :].rearrange("(p a) d -> p a d", a=TILES)
 
         warm = const.tile([P, 8], F32, name="warm")
         warm2 = const.tile([P, 8], F32, name="warm2")
@@ -60,23 +59,23 @@ def tile_attention_pa_l_kernel(tc, x, freqs_cos, freqs_sin, wq, wkv_down, wk_up,
         nc.scalar.copy(out=warm2[:], in_=warm[:])
         ident = const.tile([P, P], F32, name="ident")
         make_identity(nc, ident[:])
-        trig = const.tile([P, 3, NTILE, 64], BF16, name="trig")
+        trig = const.tile([P, 3, TILES, 64], BF16, name="trig")
 
         def load_trig():
-            nc.gpsimd.dma_start(out=trig[:, 0, :, :], in_=freqs_sin.rearrange("(p a) j -> p a j", a=NTILE))
-            nc.gpsimd.dma_start(out=trig[:, 1, :, :], in_=freqs_cos.rearrange("(p a) j -> p a j", a=NTILE))
+            nc.sync.dma_start(out=trig[:, 0, :, :], in_=freqs_sin.rearrange("(p a) j -> p a j", a=TILES))
+            nc.sync.dma_start(out=trig[:, 1, :, :], in_=freqs_cos.rearrange("(p a) j -> p a j", a=TILES))
             nc.vector.tensor_scalar(out=trig[:, 2, :, :], in0=trig[:, 0, :, :], scalar1=-1.0, scalar2=0.0, op0=MULT, op1=ADD)
 
-        wqc = [const.tile([P, NPASS, 512], U32, name="wqc%d" % c, align_bytes=64) for c in range(4)]
-        wqs = [const.tile([P, 2, 512], U8, name="wqs%d" % c, align_bytes=64) for c in range(4)]
-        kvc = [const.tile([P, NPASS, 512], U32, name="kvc%d" % g, align_bytes=64) for g in range(2)]
-        kvs = [const.tile([P, 2, 512], U8, name="kvs%d" % g, align_bytes=64) for g in range(2)]
-        upc = const.tile([P, 2, 256], U32, name="upc", align_bytes=64)
-        ups = const.tile([P, 2, 256], U8, name="ups", align_bytes=64)
-        xt = {}
+        wq_codes = [const.tile([P, PASSES, 512], U32, name="wqc%d" % c, align_bytes=64) for c in range(4)]
+        wq_scales = [const.tile([P, 2, 512], U8, name="wqs%d" % c, align_bytes=64) for c in range(4)]
+        down_codes = [const.tile([P, PASSES, 512], U32, name="kvc%d" % g, align_bytes=64) for g in range(2)]
+        down_scales = [const.tile([P, 2, 512], U8, name="kvs%d" % g, align_bytes=64) for g in range(2)]
+        up_codes = const.tile([P, 2, 256], U32, name="upc", align_bytes=64)
+        up_scales = const.tile([P, 2, 256], U8, name="ups", align_bytes=64)
+        x_tiles = {}
 
-        def plane(tile_s, g, lo, hi):
-            return tile_s[4 * (g % 4):P, g // 4, lo:hi]
+        def plane(scales, g, lo, hi):
+            return scales[4 * (g % 4):P, g // 4, lo:hi]
 
         jobs = []
 
@@ -89,357 +88,349 @@ def tile_attention_pa_l_kernel(tc, x, freqs_cos, freqs_sin, wq, wkv_down, wk_up,
                 jobs.append((kind, c, rt))
 
         add_x(0)
-        add_w("kv", 0)
-        for b in range(1, NHEAD):
+        add_w("down", 0)
+        for b in range(1, HEAD_BLOCKS):
             add_x(b)
         for rt in range(4):
             jobs.append(("wq", 0, rt))
-            jobs.append(("kv", 1, rt))
+            jobs.append(("down", 1, rt))
         jobs.append(("up", 0, 0))
         jobs.append(("up", 1, 0))
         for c in range(1, 4):
             add_w("wq", c)
-        for b in range(NHEAD, NBLK):
+        for b in range(HEAD_BLOCKS, BLOCKS):
             add_x(b)
-        nj = len(jobs)
-        jidx = {}
-        for i, j in enumerate(jobs):
-            jidx[j] = i
+        n_jobs = len(jobs)
+        job_index = {}
+        for i, job in enumerate(jobs):
+            job_index[job] = i
+        last_weight_job = job_index[("wq", 3, 3)]
 
-        first_wq = jidx[("wq", 0, 0)]
-        last_w = jidx[("wq", 3, 3)]
+        def on_vector(job):
+            return job[0] == "x" and job[1] >= HEAD_BLOCKS
 
-        def on_dve(j):
-            return j[0] == "x" and j[1] >= NDVE
-
-        def job_srcs(j):
-            kind, c, rt = j
-            if on_dve(j):
-                return [(32 * i, 32 * (i + 1), xv[:, 2 * c + rt, 1024 * i:1024 * (i + 1)].rearrange("(j b) k -> b j k", j=4)) for i in range(4)]
+        def job_sources(job):
+            kind, c, rt = job
+            if on_vector(job):
+                return [(32 * i, 32 * (i + 1), x_view[:, 2 * c + rt, 1024 * i:1024 * (i + 1)].rearrange("(j b) k -> b j k", j=4)) for i in range(4)]
             if kind == "x":
-                return [(0, P, xv[:, 2 * c + rt, :])]
-            if kind == "kv":
+                return [(0, P, x_view[:, 2 * c + rt, :])]
+            if kind == "down":
                 return [(0, P, wkv_down[512 * c + rt:512 * (c + 1):4, :])]
             if kind == "wq":
                 base = 512 * c + 256 * (rt % 2) + rt // 2
                 return [(0, P, wq[base:base + 255:2, :])]
             if c == 0:
-                return [(0, 64, wk_up[0:D:2, :]), (64, P, wk_up[1:D:2, :])]
+                return [(0, 64, wk_up[0:HEAD:2, :]), (64, P, wk_up[1:HEAD:2, :])]
             return [(0, P, wv_up[:, :])]
 
-        def job_dst(j, g):
-            kind, c, rt = j
+        def job_target(job, g):
+            kind, c, rt = job
             lo, hi = P * rt, P * (rt + 1)
             if kind == "x":
-                return xt[c][0][:, g, lo:hi], plane(xt[c][1], g, lo, hi)
-            if kind == "kv":
-                return kvc[c][:, g, lo:hi], plane(kvs[c], g, lo, hi)
+                return x_tiles[c][0][:, g, lo:hi], plane(x_tiles[c][1], g, lo, hi)
+            if kind == "down":
+                return down_codes[c][:, g, lo:hi], plane(down_scales[c], g, lo, hi)
             if kind == "wq":
-                return wqc[c][:, g, lo:hi], plane(wqs[c], g, lo, hi)
-            return upc[:, g, P * c:P * (c + 1)], ups[:, g, P * c:P * (c + 1)]
+                return wq_codes[c][:, g, lo:hi], plane(wq_scales[c], g, lo, hi)
+            return up_codes[:, g, P * c:P * (c + 1)], up_scales[:, g, P * c:P * (c + 1)]
 
-        state = {}
+        job_tiles = {}
 
-        def width(j):
-            return 1024 if j[0] == "up" else 4096
+        def k_width(job):
+            return LATENT if job[0] == "up" else K1
 
         def load(i):
-            j = jobs[i]
-            w = width(j)
-            raw = rawp.tile([P, 4096], BF16, name="raw")
-            for lo, hi, src in job_srcs(j):
-                if on_dve(j):
-                    queue = nc.scalar if lo < 64 else nc.gpsimd
-                    queue.dma_start(out=raw[lo:hi, :].rearrange("b (j k) -> b j k", j=4), in_=src)
+            job = jobs[i]
+            raw = rawp.tile([P, K1], BF16, name="raw")
+            for lo, hi, source in job_sources(job):
+                if on_vector(job):
+                    nc.sync.dma_start(out=raw[lo:hi, :].rearrange("b (j k) -> b j k", j=4), in_=source)
                 else:
-                    nc.sync.dma_start(out=raw[lo:hi, 0:w], in_=src)
-            state[i] = {"raw": raw}
+                    nc.sync.dma_start(out=raw[lo:hi, 0:k_width(job)], in_=source)
+            job_tiles[i] = {"raw": raw}
 
-        def sort(i, half):
-            w = width(jobs[i]) // 2
-            if half == 0:
-                srt_new = srtp.tile([P, 2048], F32, name="srt", align_bytes=64)
-                state[i]["srt"] = srt_new
-            srt = state[i]["srt"]
-            words = state[i]["raw"][:, 0:2 * w].bitcast(F32)
-            if jobs[i][0] == "up" and half == 1:
+        def sort(i, u):
+            job = jobs[i]
+            if u == 0:
+                srt_new = srtp.tile([P, K1 // 2], F32, name="srt", align_bytes=64)
+                job_tiles[i]["srt"] = srt_new
+            srt = job_tiles[i]["srt"]
+            words = job_tiles[i]["raw"][:, 0:k_width(job)].bitcast(F32)
+            if job[0] == "up" and u == 1:
                 return
-            if jobs[i][0] == "up":
+            if job[0] == "up":
                 nc.vector.tensor_copy(
                     out=srt[:].rearrange("r (u g p) -> r g u p", u=2, p=P)[:, 0:2, :, :],
                     in_=words.rearrange("r (g p u) -> r g u p", u=2, p=P),
                 )
+                return
+            target = srt[:, 1024 * u:1024 * (u + 1)].rearrange("r (g m s) -> r g m s", m=16, s=8)
+            source = words.rearrange("r (m g u s) -> r u g m s", g=8, u=2, s=8)[:, u, :, :, :]
+            if i <= last_weight_job:
+                nc.vector.tensor_copy(out=target, in_=source)
             else:
-                for u in range(half, half + 1):
-                    dst = srt[:, 1024 * u:1024 * (u + 1)].rearrange("r (g m s) -> r g m s", m=16, s=8)
-                    src = words.rearrange("r (m g u s) -> r u g m s", g=8, u=2, s=8)[:, u, :, :, :]
-                    if i <= last_w:
-                        nc.vector.tensor_copy(out=dst, in_=src)
-                    else:
-                        nc.scalar.copy(out=dst, in_=src)
+                nc.scalar.copy(out=target, in_=source)
 
         def job_steps(i):
-            j = jobs[i]
-            nbank = width(j) // 1024
-            st = state[i]
+            job = jobs[i]
+            n_banks = k_width(job) // 1024
+            tiles = job_tiles[i]
             turned = []
-            grps = {}
-            out = []
+            woven = {}
 
             def begin():
-                if i + AHEAD < nj:
-                    load(i + AHEAD)
-                if i == 4:
+                if i + LOADS_AHEAD < n_jobs:
+                    load(i + LOADS_AHEAD)
+                if i == TRIG_JOB:
                     load_trig()
-                if j[0] == "x" and j[2] == 0:
-                    xc_new = xpool.tile([P, NPASS, 256], U32, name="xc", align_bytes=64)
+                if job[0] == "x" and job[2] == 0:
+                    xc_new = xpool.tile([P, PASSES, 256], U32, name="xc", align_bytes=64)
                     xs_new = xpool.tile([P, 2, 256], U8, name="xs", align_bytes=64)
-                    xt[j[1]] = (xc_new, xs_new)
-                srt = st["srt"]
-                if on_dve(j):
-                    tr = onep.tile([P, 2048], F32, name="tr", align_bytes=64)
-                    st["tr"] = tr
+                    x_tiles[job[1]] = (xc_new, xs_new)
+                srt = tiles["srt"]
+                if on_vector(job):
+                    tr = onep.tile([P, K1 // 2], F32, name="tr", align_bytes=64)
+                    tiles["tr"] = tr
                     nc.vector.transpose(out=tr[:, 0:1024], in_=srt[:, 0:1024])
-                    for bk in range(nbank):
-                        turned.append(tr[:].rearrange("p (u g r) -> p g r u", u=2, g=8)[:, 2 * bk:2 * bk + 2, :, :])
+                    for bank in range(n_banks):
+                        turned.append(tr[:].rearrange("p (u g r) -> p g r u", u=2, g=8)[:, 2 * bank:2 * bank + 2, :, :])
                 else:
-                    for bk in range(nbank):
-                        tb = pst.tile([P, 512], F32, name="tb")
-                        for s in range(4):
-                            col = 1024 * (s % 2) + P * (2 * bk + s // 2)
-                            nc.tensor.transpose(out=tb[:, P * s:P * (s + 1)], in_=srt[:, col:col + P], identity=ident[:])
+                    for bank in range(n_banks):
+                        tb = psa.tile([P, 512], F32, name="acc")
+                        for slot in range(4):
+                            col = 1024 * (slot % 2) + P * (2 * bank + slot // 2)
+                            nc.tensor.transpose(out=tb[:, P * slot:P * (slot + 1)], in_=srt[:, col:col + P], identity=ident[:])
                         turned.append(tb[:].rearrange("p (g u r) -> p g r u", g=2, u=2))
 
-            def second_half():
-                nc.vector.transpose(out=st["tr"][:, 1024:2048], in_=st["srt"][:, 1024:2048])
+            def turn_second_half():
+                nc.vector.transpose(out=tiles["tr"][:, 1024:2048], in_=tiles["srt"][:, 1024:2048])
 
-            def weave_bank(bk):
+            def weave(bank):
                 grp = grpp.tile([P, 512], F32, name="grp", align_bytes=64)
-                nc.scalar.copy(out=grp[:].rearrange("p (g r u) -> p g r u", g=2, u=2), in_=turned[bk])
-                grps[bk] = grp
+                nc.scalar.copy(out=grp[:].rearrange("p (g r u) -> p g r u", g=2, u=2), in_=turned[bank])
+                woven[bank] = grp
 
-            def quant_bank(bk):
+            def quantize(bank):
                 for g2 in range(2):
-                    g = 2 * bk + g2
-                    codes, scl = job_dst(j, g)
-                    nc.vector.quantize_mx(out=codes.bitcast(FP8X4), scales=scl, in_=grps[bk][:].bitcast(BF16)[:, 512 * g2:512 * (g2 + 1)])
+                    codes, scales = job_target(job, 2 * bank + g2)
+                    nc.vector.quantize_mx(out=codes.bitcast(FP8X4), scales=scales, in_=woven[bank][:].bitcast(BF16)[:, 512 * g2:512 * (g2 + 1)])
 
-            def sort_next(half):
+            def sort_next(u):
                 def run():
-                    sort(i + 1, half)
+                    sort(i + 1, u)
                 return run
 
-            def bank_step(bk):
+            def bank_step(bank):
                 def run():
-                    if bk + 1 < nbank:
-                        weave_bank(bk + 1)
-                    if bk >= 0:
-                        quant_bank(bk)
+                    if bank + 2 < n_banks:
+                        weave(bank + 2)
+                    if bank >= 0:
+                        quantize(bank)
                 return run
 
-            out.append(begin)
-            if on_dve(j):
-                out.append(second_half)
-            if i + 1 < nj:
-                out.append(sort_next(0))
-                out.append(sort_next(1))
-            for bk in range(-1, nbank):
-                out.append(bank_step(bk))
-            return out
+            steps_of_job = [begin]
+            if on_vector(job):
+                steps_of_job.append(turn_second_half)
+            if i + 1 < n_jobs:
+                steps_of_job.append(sort_next(0))
+                steps_of_job.append(sort_next(1))
+            for bank in range(-2, n_banks):
+                steps_of_job.append(bank_step(bank))
+            return steps_of_job
 
-        later = []
+        deferred = []
 
         def flush():
-            n = len(later)
-            for i in range(n):
-                later.pop(0)()
+            for n in range(len(deferred)):
+                deferred.pop(0)()
 
         def unit_q(b, a1, c):
             a = 2 * b + a1
-            xc, xs = xt[b]
+            xc, xs = x_tiles[b]
             acc = psa.tile([P, 512], F32, name="acc")
-            for g in range(NPASS):
+            for g in range(PASSES):
                 nc.tensor.matmul_mx(
                     out=acc[:],
                     lhsT=xc[:, g, P * a1:P * (a1 + 1)].bitcast(FP8X4), lhsT_scale=plane(xs, g, P * a1, P * (a1 + 1)),
-                    rhs=wqc[c][:, g, :].bitcast(FP8X4), rhs_scale=plane(wqs[c], g, 0, 512),
-                    start=(g == 0), stop=(g == NPASS - 1),
+                    rhs=wq_codes[c][:, g, :].bitcast(FP8X4), rhs_scale=plane(wq_scales[c], g, 0, 512),
+                    start=(g == 0), stop=(g == PASSES - 1),
                 )
-            pr = ropep.tile([P, 2, 2, 256], F32, name="pr")
-            av = acc[:].rearrange("p (e h j) -> p e h j", e=2, h=4)
+            pr = onep.tile([P, 2, 2, 256], F32, name="pr")
+            halves = acc[:].rearrange("p (e h j) -> p e h j", e=2, h=4)
             for e1 in range(2):
-                tg = trig[:, 1 - e1:3 - e1, a, :].unsqueeze(2).to_broadcast([P, 2, 4, 64])
-                nc.vector.tensor_tensor(out=pr[:, e1, :, :].rearrange("p e (h j) -> p e h j", h=4), in0=av, in1=tg, op=MULT)
+                factors = trig[:, 1 - e1:3 - e1, a, :].unsqueeze(2).to_broadcast([P, 2, 4, 64])
+                nc.vector.tensor_tensor(out=pr[:, e1, :, :].rearrange("p e (h j) -> p e h j", h=4), in0=halves, in1=factors, op=MULT)
+            oo = ropep.tile([P, 2, 256], F32, name="oo")
+            for e1 in range(2):
+                nc.vector.tensor_tensor(out=oo[:, e1, :], in0=pr[:, e1, 0, :], in1=pr[:, e1, 1, :], op=ADD)
             flush()
 
-            def fin():
+            def interleave_and_store():
                 ost = outp.tile([P, 512], F32, name="ost")
-                nc.gpsimd.tensor_tensor(
-                    out=ost[:].rearrange("p (m e) -> p m e", e=2),
-                    in0=pr[:, :, 0, :].rearrange("p e m -> p m e"), in1=pr[:, :, 1, :].rearrange("p e m -> p m e"), op=ADD,
-                )
-                nc.sync.dma_start(out=qv[:, a, 512 * c:512 * (c + 1)], in_=ost[:])
-            later.append(fin)
+                nc.scalar.copy(out=ost[:].rearrange("p (m e) -> p m e", e=2), in_=oo[:].rearrange("p e m -> p m e"))
+                nc.sync.dma_start(out=q_view[:, a, 512 * c:512 * (c + 1)], in_=ost[:])
+            deferred.append(interleave_and_store)
 
-        lat = {}
+        latent = {}
 
-        def unit_l(b, gg, q):
-            xc, xs = xt[b]
+        def unit_latent(b, big_g, pair):
+            xc, xs = x_tiles[b]
             acc = psa.tile([P, 512], F32, name="acc")
             for t2 in range(2):
-                t = 2 * q + t2
-                for g in range(NPASS):
+                t = 2 * pair + t2
+                for g in range(PASSES):
                     nc.tensor.matmul_mx(
                         out=acc[:, 256 * t2:256 * (t2 + 1)],
-                        lhsT=kvc[gg][:, g, P * t:P * (t + 1)].bitcast(FP8X4), lhsT_scale=plane(kvs[gg], g, P * t, P * (t + 1)),
+                        lhsT=down_codes[big_g][:, g, P * t:P * (t + 1)].bitcast(FP8X4), lhsT_scale=plane(down_scales[big_g], g, P * t, P * (t + 1)),
                         rhs=xc[:, g, :].bitcast(FP8X4), rhs_scale=plane(xs, g, 0, 256),
-                        start=(g == 0), stop=(g == NPASS - 1),
+                        start=(g == 0), stop=(g == PASSES - 1),
                     )
             flush()
-            if q == 0:
+            if pair == 0:
                 lat4_new = latp.tile([P, 4, 256], BF16, name="lat4")
-                lat[(b, gg)] = lat4_new
-            if q == 0 and gg == 0:
+                latent[(b, big_g)] = lat4_new
+            if pair == 0 and big_g == 0:
                 latc_new = latcp.tile([P, 2, 256], U32, name="latc", align_bytes=64)
                 lats_new = latcp.tile([P, 2, 256], U8, name="lats", align_bytes=64)
-                lat[b] = (latc_new, lats_new)
-            lat4 = lat[(b, gg)]
+                latent[b] = (latc_new, lats_new)
+            lat4 = latent[(b, big_g)]
 
-            def quant():
-                gl = lat[(b, gg, "gl")]
-                nc.vector.quantize_mx(out=lat[b][0][:, gg, :].bitcast(FP8X4), scales=lat[b][1][:, gg, :], in_=gl[:])
+            def quantize_latent():
+                nc.vector.quantize_mx(out=latent[b][0][:, big_g, :].bitcast(FP8X4), scales=latent[b][1][:, big_g, :], in_=latent[(b, big_g, "gl")][:])
 
-            def weave():
+            def interleave_latent():
                 gl = onep.tile([P, 1024], BF16, name="gl", align_bytes=64)
-                lat[(b, gg, "gl")] = gl
-                if b < NHEAD:
+                latent[(b, big_g, "gl")] = gl
+                if b < HEAD_BLOCKS:
                     nc.vector.tensor_copy(out=gl[:].rearrange("p (n t) -> p n t", t=4), in_=lat4[:].rearrange("p t n -> p n t"))
                 else:
                     nc.scalar.copy(out=gl[:].rearrange("p (n t) -> p n t", t=4), in_=lat4[:].rearrange("p t n -> p n t"))
-                later.append(quant)
+                deferred.append(quantize_latent)
 
-            def out_of_psum():
-                nc.scalar.copy(out=lat4[:, 2 * q:2 * q + 2, :], in_=acc[:].rearrange("p (t n) -> p t n", t=2))
-                if q == 1:
-                    later.append(weave)
-            later.append(out_of_psum)
+            def round_latent():
+                nc.scalar.copy(out=lat4[:, 2 * pair:2 * pair + 2, :], in_=acc[:].rearrange("p (t n) -> p t n", t=2))
+                if pair == 1:
+                    deferred.append(interleave_latent)
+            deferred.append(round_latent)
 
-        def unit_s2(b):
-            while len(later) > 0:
+        def unit_kv(b):
+            while len(deferred) > 0:
                 flush()
-            latc, lats = lat[b]
+            latc, lats = latent[b]
             acc = psa.tile([P, 512], F32, name="acc")
             for a1 in range(2):
-                for gg in range(2):
+                for big_g in range(2):
                     nc.tensor.matmul_mx(
                         out=acc[:, 256 * a1:256 * (a1 + 1)],
-                        lhsT=latc[:, gg, P * a1:P * (a1 + 1)].bitcast(FP8X4), lhsT_scale=lats[:, gg, P * a1:P * (a1 + 1)],
-                        rhs=upc[:, gg, :].bitcast(FP8X4), rhs_scale=ups[:, gg, :],
-                        start=(gg == 0), stop=(gg == 1),
+                        lhsT=latc[:, big_g, P * a1:P * (a1 + 1)].bitcast(FP8X4), lhsT_scale=lats[:, big_g, P * a1:P * (a1 + 1)],
+                        rhs=up_codes[:, big_g, :].bitcast(FP8X4), rhs_scale=up_scales[:, big_g, :],
+                        start=(big_g == 0), stop=(big_g == 1),
                     )
-            av = acc[:].rearrange("p (a s e j) -> p a s e j", a=2, s=2, e=2)
+            parts = acc[:].rearrange("p (a s e j) -> p a s e j", a=2, s=2, e=2)
             prk = kvp.tile([P, 2, 2, 2, 64], F32, name="prk")
             for e1 in range(2):
-                tg = trig[:, 1 - e1:3 - e1, 2 * b:2 * b + 2, :].rearrange("p e a j -> p a e j")
-                nc.vector.tensor_tensor(out=prk[:, e1, :, :, :], in0=av[:, :, 0, :, :], in1=tg, op=MULT)
+                factors = trig[:, 1 - e1:3 - e1, 2 * b:2 * b + 2, :].rearrange("p e a j -> p a e j")
+                nc.vector.tensor_tensor(out=prk[:, e1, :, :, :], in0=parts[:, :, 0, :, :], in1=factors, op=MULT)
             ok = kvp.tile([P, 2, 2, 64], F32, name="ok")
-            nc.vector.tensor_tensor(out=ok[:], in0=prk[:, :, :, 0, :], in1=prk[:, :, :, 1, :], op=ADD)
-            vst = kvp.tile([P, 2, D], F32, name="vst")
+            vst = kvp.tile([P, 2, HEAD], F32, name="vst")
             nc.vector.tensor_copy(out=vst[:], in_=acc[:].rearrange("p (a s d) -> p a s d", a=2, s=2)[:, :, 1, :])
+            nc.vector.tensor_tensor(out=ok[:], in0=prk[:, :, :, 0, :], in1=prk[:, :, :, 1, :], op=ADD)
             flush()
 
-            def fin():
-                kst = kvp.tile([P, 2, D], F32, name="kst")
+            def interleave_and_store():
+                kst = kvp.tile([P, 2, HEAD], F32, name="kst")
                 nc.scalar.copy(out=kst[:].rearrange("p a (j e) -> p a j e", e=2), in_=ok[:].rearrange("p e a j -> p a j e"))
-                nc.sync.dma_start(out=kv[:, 2 * b:2 * b + 2, :], in_=kst[:])
-                nc.sync.dma_start(out=vv[:, 2 * b:2 * b + 2, :], in_=vst[:])
-            later.append(fin)
+                nc.sync.dma_start(out=k_view[:, 2 * b:2 * b + 2, :], in_=kst[:])
+                nc.sync.dma_start(out=v_view[:, 2 * b:2 * b + 2, :], in_=vst[:])
+            deferred.append(interleave_and_store)
 
-        def need(u):
-            kind, b, i1, i2 = u
+        def last_job_read(unit):
+            kind, b, i1, i2 = unit
             if kind == "Q":
-                return max(jidx[("x", b, i1)], jidx[("wq", i2, 3)])
+                return max(job_index[("x", b, i1)], job_index[("wq", i2, 3)])
             if kind == "L":
-                return max(jidx[("x", b, 1)], jidx[("kv", i1, 2 * i2 + 1)])
-            return jidx[("up", 1, 0)]
+                return max(job_index[("x", b, 1)], job_index[("down", i1, 2 * i2 + 1)])
+            return job_index[("up", 1, 0)]
 
         units = []
-        for gg in range(2):
-            for b in range(NHEAD):
-                units.append(("L", b, gg, 0))
-                units.append(("L", b, gg, 1))
+        for big_g in range(2):
+            for b in range(HEAD_BLOCKS):
+                units.append(("L", b, big_g, 0))
+                units.append(("L", b, big_g, 1))
         for c in range(4):
-            for b in range(NHEAD):
+            for b in range(HEAD_BLOCKS):
                 units.append(("Q", b, 0, c))
                 units.append(("Q", b, 1, c))
-        units.sort(key=need)
-        at = units.index(("Q", 0, 0, 1))
-        for b in range(NHEAD):
-            units.insert(at + 3 * b + 2, ("S", b, 0, 0))
+        units.sort(key=last_job_read)
+        first = units.index(("Q", 0, 0, 1))
+        for b in range(HEAD_BLOCKS):
+            units.insert(first + 3 * b + 2, ("KV", b, 0, 0))
         for c in range(4):
-            units.append(("Q", NHEAD, 0, c))
+            units.append(("Q", HEAD_BLOCKS, 0, c))
         for s in range(4):
-            units.append(("L", NHEAD, s // 2, s % 2))
+            units.append(("L", HEAD_BLOCKS, s // 2, s % 2))
         for c in range(4):
-            units.append(("Q", NHEAD, 1, c))
-        for b in range(NHEAD + 1, NBLK - 1):
+            units.append(("Q", HEAD_BLOCKS, 1, c))
+        for b in range(HEAD_BLOCKS + 1, BLOCKS - 1):
             for s in range(4):
                 units.append(("L", b, s // 2, s % 2))
                 units.append(("Q", b, s // 2, 2 * (s % 2)))
                 units.append(("Q", b, s // 2, 2 * (s % 2) + 1))
                 if s == 0:
-                    units.append(("S", b - 1, 0, 0))
-        b = NBLK - 1
+                    units.append(("KV", b - 1, 0, 0))
+        b = BLOCKS - 1
         for s in range(4):
             units.append(("L", b, s // 2, s % 2))
-        units.append(("S", b - 1, 0, 0))
+        units.append(("KV", b - 1, 0, 0))
         for s in range(8):
             units.append(("Q", b, s // 4, s % 4))
             if s == 3:
-                units.append(("S", b, 0, 0))
-
+                units.append(("KV", b, 0, 0))
+        n_units = len(units)
 
         last_unit = {}
-        for i, u in enumerate(units):
-            if u[0] != "S":
-                last_unit[u[1]] = i
+        for i, unit in enumerate(units):
+            if unit[0] != "KV":
+                last_unit[unit[1]] = i
 
-        def gate(j):
-            if j[0] == "x" and j[1] >= NXB:
-                return last_unit[j[1] - NXB] + 1
+        def units_before(job):
+            if job[0] == "x" and job[1] >= X_BUFFERS:
+                return last_unit[job[1] - X_BUFFERS] + 1
             return 0
 
-        nu = len(units)
-        for i in range(AHEAD):
+        for i in range(LOADS_AHEAD):
             load(i)
         sort(0, 0)
         sort(0, 1)
         steps = []
-        js, uu = 0, 0
-        while js < nj or uu < nu or len(steps) > 0:
+        jobs_begun, units_done = 0, 0
+        while jobs_begun < n_jobs or units_done < n_units or len(steps) > 0:
             moved = False
-            if len(steps) == 0 and js < nj and gate(jobs[js]) <= uu:
-                steps.extend(job_steps(js))
-                js += 1
-            done = js if len(steps) == 0 else js - 1
-            held = len(steps) == 0
-            if uu < nu and need(units[uu]) + (0 if held else LAG) < done:
-                kind, b, i1, i2 = units[uu]
+            wrote_unit = False
+            if len(steps) == 0 and jobs_begun < n_jobs and units_before(jobs[jobs_begun]) <= units_done:
+                steps.extend(job_steps(jobs_begun))
+                jobs_begun += 1
+            between_jobs = len(steps) == 0
+            jobs_done = jobs_begun if between_jobs else jobs_begun - 1
+            if units_done < n_units and last_job_read(units[units_done]) + (0 if between_jobs else JOB_LAG) < jobs_done:
+                kind, b, i1, i2 = units[units_done]
                 if kind == "Q":
                     unit_q(b, i1, i2)
                 elif kind == "L":
-                    unit_l(b, i1, i2)
+                    unit_latent(b, i1, i2)
                 else:
-                    unit_s2(b)
-                uu += 1
+                    unit_kv(b)
+                units_done += 1
                 moved = True
-            n = SPU if js > last_w + 3 else SPU_HEAD
+                wrote_unit = True
+            n = STEPS_PER_UNIT if jobs_begun > last_weight_job + 3 else STEPS_PER_UNIT_HEAD
             while n > 0 and len(steps) > 0:
                 steps.pop(0)()
                 n -= 1
                 moved = True
-            if not moved:
+            if not wrote_unit:
                 flush()
-            assert moved or len(later) > 0 or uu < nu
-        while len(later) > 0:
+            assert moved or len(deferred) > 0 or units_done < n_units
+        while len(deferred) > 0:
             flush()

from contextlib import ExitStack

import concourse.mybir as mybir
from concourse.masks import make_identity

F32 = mybir.dt.float32
BF16 = mybir.dt.bfloat16
U32 = mybir.dt.uint32
U8 = mybir.dt.uint8
FP8X4 = mybir.dt.float8_e4m3fn_x4
MULT = mybir.AluOpType.mult
ADD = mybir.AluOpType.add

P = 128
TOKENS = 4096
K1 = 4096
Q_CHANNELS = 2048
LATENT = 1024
HEAD = 128
PASSES = K1 // 512
TILES = TOKENS // P
BLOCKS = TILES // 2
FLOPS = 2 * TOKENS * K1 * (Q_CHANNELS + LATENT) + 2 * TOKENS * LATENT * 2 * HEAD

X_BUFFERS = 3
HEAD_BLOCKS = 3
LOADS_AHEAD = 2
JOB_LAG = 1
TRIG_JOB = 12
STEPS_PER_UNIT = 2
STEPS_PER_UNIT_HEAD = 5


def tile_attention_pa_l_kernel(tc, x, freqs_cos, freqs_sin, wq, wkv_down, wk_up, wv_up, out_0, out_1, out_2):
    nc = tc.nc
    with ExitStack() as ctx:
        const = ctx.enter_context(tc.tile_pool(name="const", bufs=1))
        xpool = ctx.enter_context(tc.tile_pool(name="xpool", bufs=X_BUFFERS))
        rawp = ctx.enter_context(tc.tile_pool(name="rawp", bufs=LOADS_AHEAD + 1))
        srtp = ctx.enter_context(tc.tile_pool(name="srtp", bufs=2))
        onep = ctx.enter_context(tc.tile_pool(name="onep", bufs=1))
        grpp = ctx.enter_context(tc.tile_pool(name="grpp", bufs=4))
        latp = ctx.enter_context(tc.tile_pool(name="latp", bufs=HEAD_BLOCKS))
        latcp = ctx.enter_context(tc.tile_pool(name="latcp", bufs=HEAD_BLOCKS))
        kvp = ctx.enter_context(tc.tile_pool(name="kvp", bufs=1))
        ropep = ctx.enter_context(tc.tile_pool(name="ropep", bufs=2))
        outp = ctx.enter_context(tc.tile_pool(name="outp", bufs=4))
        psa = ctx.enter_context(tc.psum_pool(name="psa", bufs=8))
        ctx.enter_context(tc.manual_schedule())

        x_view = x[0, :, :].rearrange("(p a) k -> p a k", a=TILES)
        q_view = out_0[0, :, :, :].rearrange("(p a) h d -> p a (h d)", a=TILES)
        k_view = out_1[0, :, :].rearrange("(p a) d -> p a d", a=TILES)
        v_view = out_2[0, :, :].rearrange("(p a) d -> p a d", a=TILES)

        warm = const.tile([P, 8], F32, name="warm")
        warm2 = const.tile([P, 8], F32, name="warm2")
        nc.vector.memset(warm[:], 0.0)
        nc.scalar.copy(out=warm2[:], in_=warm[:])
        ident = const.tile([P, P], F32, name="ident")
        make_identity(nc, ident[:])
        trig = const.tile([P, 3, TILES, 64], BF16, name="trig")

        def load_trig():
            nc.sync.dma_start(out=trig[:, 0, :, :], in_=freqs_sin.rearrange("(p a) j -> p a j", a=TILES))
            nc.sync.dma_start(out=trig[:, 1, :, :], in_=freqs_cos.rearrange("(p a) j -> p a j", a=TILES))
            nc.vector.tensor_scalar(out=trig[:, 2, :, :], in0=trig[:, 0, :, :], scalar1=-1.0, scalar2=0.0, op0=MULT, op1=ADD)

        wq_codes = [const.tile([P, PASSES, 512], U32, name="wqc%d" % c, align_bytes=64) for c in range(4)]
        wq_scales = [const.tile([P, 2, 512], U8, name="wqs%d" % c, align_bytes=64) for c in range(4)]
        down_codes = [const.tile([P, PASSES, 512], U32, name="kvc%d" % g, align_bytes=64) for g in range(2)]
        down_scales = [const.tile([P, 2, 512], U8, name="kvs%d" % g, align_bytes=64) for g in range(2)]
        up_codes = const.tile([P, 2, 256], U32, name="upc", align_bytes=64)
        up_scales = const.tile([P, 2, 256], U8, name="ups", align_bytes=64)
        x_tiles = {}

        def plane(scales, g, lo, hi):
            return scales[4 * (g % 4):P, g // 4, lo:hi]

        jobs = []

        def add_x(b):
            for a1 in range(2):
                jobs.append(("x", b, a1))

        def add_w(kind, c):
            for rt in range(4):
                jobs.append((kind, c, rt))

        add_x(0)
        add_w("down", 0)
        for b in range(1, HEAD_BLOCKS):
            add_x(b)
        for rt in range(4):
            jobs.append(("wq", 0, rt))
            jobs.append(("down", 1, rt))
        jobs.append(("up", 0, 0))
        jobs.append(("up", 1, 0))
        for c in range(1, 4):
            add_w("wq", c)
        for b in range(HEAD_BLOCKS, BLOCKS):
            add_x(b)
        n_jobs = len(jobs)
        job_index = {}
        for i, job in enumerate(jobs):
            job_index[job] = i
        last_weight_job = job_index[("wq", 3, 3)]

        def on_vector(job):
            return job[0] == "x" and job[1] >= HEAD_BLOCKS

        def job_sources(job):
            kind, c, rt = job
            if on_vector(job):
                return [(32 * i, 32 * (i + 1), x_view[:, 2 * c + rt, 1024 * i:1024 * (i + 1)].rearrange("(j b) k -> b j k", j=4)) for i in range(4)]
            if kind == "x":
                return [(0, P, x_view[:, 2 * c + rt, :])]
            if kind == "down":
                return [(0, P, wkv_down[512 * c + rt:512 * (c + 1):4, :])]
            if kind == "wq":
                base = 512 * c + 256 * (rt % 2) + rt // 2
                return [(0, P, wq[base:base + 255:2, :])]
            if c == 0:
                return [(0, 64, wk_up[0:HEAD:2, :]), (64, P, wk_up[1:HEAD:2, :])]
            return [(0, P, wv_up[:, :])]

        def job_target(job, g):
            kind, c, rt = job
            lo, hi = P * rt, P * (rt + 1)
            if kind == "x":
                return x_tiles[c][0][:, g, lo:hi], plane(x_tiles[c][1], g, lo, hi)
            if kind == "down":
                return down_codes[c][:, g, lo:hi], plane(down_scales[c], g, lo, hi)
            if kind == "wq":
                return wq_codes[c][:, g, lo:hi], plane(wq_scales[c], g, lo, hi)
            return up_codes[:, g, P * c:P * (c + 1)], up_scales[:, g, P * c:P * (c + 1)]

        job_tiles = {}

        def k_width(job):
            return LATENT if job[0] == "up" else K1

        def load(i):
            job = jobs[i]
            raw = rawp.tile([P, K1], BF16, name="raw")
            for lo, hi, source in job_sources(job):
                if on_vector(job):
                    nc.sync.dma_start(out=raw[lo:hi, :].rearrange("b (j k) -> b j k", j=4), in_=source)
                else:
                    nc.sync.dma_start(out=raw[lo:hi, 0:k_width(job)], in_=source)
            job_tiles[i] = {"raw": raw}

        def sort(i, u):
            job = jobs[i]
            if u == 0:
                srt_new = srtp.tile([P, K1 // 2], F32, name="srt", align_bytes=64)
                job_tiles[i]["srt"] = srt_new
            srt = job_tiles[i]["srt"]
            words = job_tiles[i]["raw"][:, 0:k_width(job)].bitcast(F32)
            if job[0] == "up" and u == 1:
                return
            if job[0] == "up":
                nc.vector.tensor_copy(
                    out=srt[:].rearrange("r (u g p) -> r g u p", u=2, p=P)[:, 0:2, :, :],
                    in_=words.rearrange("r (g p u) -> r g u p", u=2, p=P),
                )
                return
            target = srt[:, 1024 * u:1024 * (u + 1)].rearrange("r (g m s) -> r g m s", m=16, s=8)
            source = words.rearrange("r (m g u s) -> r u g m s", g=8, u=2, s=8)[:, u, :, :, :]
            if i <= last_weight_job:
                nc.vector.tensor_copy(out=target, in_=source)
            else:
                nc.scalar.copy(out=target, in_=source)

        def job_steps(i):
            job = jobs[i]
            n_banks = k_width(job) // 1024
            tiles = job_tiles[i]
            turned = []
            woven = {}

            def begin():
                if i + LOADS_AHEAD < n_jobs:
                    load(i + LOADS_AHEAD)
                if i == TRIG_JOB:
                    load_trig()
                if job[0] == "x" and job[2] == 0:
                    xc_new = xpool.tile([P, PASSES, 256], U32, name="xc", align_bytes=64)
                    xs_new = xpool.tile([P, 2, 256], U8, name="xs", align_bytes=64)
                    x_tiles[job[1]] = (xc_new, xs_new)
                srt = tiles["srt"]
                if on_vector(job):
                    tr = onep.tile([P, K1 // 2], F32, name="tr", align_bytes=64)
                    tiles["tr"] = tr
                    nc.vector.transpose(out=tr[:, 0:1024], in_=srt[:, 0:1024])
                    for bank in range(n_banks):
                        turned.append(tr[:].rearrange("p (u g r) -> p g r u", u=2, g=8)[:, 2 * bank:2 * bank + 2, :, :])
                else:
                    for bank in range(n_banks):
                        tb = psa.tile([P, 512], F32, name="acc")
                        for slot in range(4):
                            col = 1024 * (slot % 2) + P * (2 * bank + slot // 2)
                            nc.tensor.transpose(out=tb[:, P * slot:P * (slot + 1)], in_=srt[:, col:col + P], identity=ident[:])
                        turned.append(tb[:].rearrange("p (g u r) -> p g r u", g=2, u=2))

            def turn_second_half():
                nc.vector.transpose(out=tiles["tr"][:, 1024:2048], in_=tiles["srt"][:, 1024:2048])

            def weave(bank):
                grp = grpp.tile([P, 512], F32, name="grp", align_bytes=64)
                nc.scalar.copy(out=grp[:].rearrange("p (g r u) -> p g r u", g=2, u=2), in_=turned[bank])
                woven[bank] = grp

            def quantize(bank):
                for g2 in range(2):
                    codes, scales = job_target(job, 2 * bank + g2)
                    nc.vector.quantize_mx(out=codes.bitcast(FP8X4), scales=scales, in_=woven[bank][:].bitcast(BF16)[:, 512 * g2:512 * (g2 + 1)])

            def sort_next(u):
                def run():
                    sort(i + 1, u)
                return run

            def bank_step(bank):
                def run():
                    if bank + 2 < n_banks:
                        weave(bank + 2)
                    if bank >= 0:
                        quantize(bank)
                return run

            steps_of_job = [begin]
            if on_vector(job):
                steps_of_job.append(turn_second_half)
            if i + 1 < n_jobs:
                steps_of_job.append(sort_next(0))
                steps_of_job.append(sort_next(1))
            for bank in range(-2, n_banks):
                steps_of_job.append(bank_step(bank))
            return steps_of_job

        deferred = []

        def flush():
            for n in range(len(deferred)):
                deferred.pop(0)()

        def unit_q(b, a1, c):
            a = 2 * b + a1
            xc, xs = x_tiles[b]
            acc = psa.tile([P, 512], F32, name="acc")
            for g in range(PASSES):
                nc.tensor.matmul_mx(
                    out=acc[:],
                    lhsT=xc[:, g, P * a1:P * (a1 + 1)].bitcast(FP8X4), lhsT_scale=plane(xs, g, P * a1, P * (a1 + 1)),
                    rhs=wq_codes[c][:, g, :].bitcast(FP8X4), rhs_scale=plane(wq_scales[c], g, 0, 512),
                    start=(g == 0), stop=(g == PASSES - 1),
                )
            pr = onep.tile([P, 2, 2, 256], F32, name="pr")
            halves = acc[:].rearrange("p (e h j) -> p e h j", e=2, h=4)
            for e1 in range(2):
                factors = trig[:, 1 - e1:3 - e1, a, :].unsqueeze(2).to_broadcast([P, 2, 4, 64])
                nc.vector.tensor_tensor(out=pr[:, e1, :, :].rearrange("p e (h j) -> p e h j", h=4), in0=halves, in1=factors, op=MULT)
            oo = ropep.tile([P, 2, 256], F32, name="oo")
            for e1 in range(2):
                nc.vector.tensor_tensor(out=oo[:, e1, :], in0=pr[:, e1, 0, :], in1=pr[:, e1, 1, :], op=ADD)
            flush()

            def interleave_and_store():
                ost = outp.tile([P, 512], F32, name="ost")
                nc.scalar.copy(out=ost[:].rearrange("p (m e) -> p m e", e=2), in_=oo[:].rearrange("p e m -> p m e"))
                nc.sync.dma_start(out=q_view[:, a, 512 * c:512 * (c + 1)], in_=ost[:])
            deferred.append(interleave_and_store)

        latent = {}

        def unit_latent(b, big_g, pair):
            xc, xs = x_tiles[b]
            acc = psa.tile([P, 512], F32, name="acc")
            for t2 in range(2):
                t = 2 * pair + t2
                for g in range(PASSES):
                    nc.tensor.matmul_mx(
                        out=acc[:, 256 * t2:256 * (t2 + 1)],
                        lhsT=down_codes[big_g][:, g, P * t:P * (t + 1)].bitcast(FP8X4), lhsT_scale=plane(down_scales[big_g], g, P * t, P * (t + 1)),
                        rhs=xc[:, g, :].bitcast(FP8X4), rhs_scale=plane(xs, g, 0, 256),
                        start=(g == 0), stop=(g == PASSES - 1),
                    )
            flush()
            if pair == 0:
                lat4_new = latp.tile([P, 4, 256], BF16, name="lat4")
                latent[(b, big_g)] = lat4_new
            if pair == 0 and big_g == 0:
                latc_new = latcp.tile([P, 2, 256], U32, name="latc", align_bytes=64)
                lats_new = latcp.tile([P, 2, 256], U8, name="lats", align_bytes=64)
                latent[b] = (latc_new, lats_new)
            lat4 = latent[(b, big_g)]

            def quantize_latent():
                nc.vector.quantize_mx(out=latent[b][0][:, big_g, :].bitcast(FP8X4), scales=latent[b][1][:, big_g, :], in_=latent[(b, big_g, "gl")][:])

            def interleave_latent():
                gl = onep.tile([P, 1024], BF16, name="gl", align_bytes=64)
                latent[(b, big_g, "gl")] = gl
                if b < HEAD_BLOCKS:
                    nc.vector.tensor_copy(out=gl[:].rearrange("p (n t) -> p n t", t=4), in_=lat4[:].rearrange("p t n -> p n t"))
                else:
                    nc.scalar.copy(out=gl[:].rearrange("p (n t) -> p n t", t=4), in_=lat4[:].rearrange("p t n -> p n t"))
                deferred.append(quantize_latent)

            def round_latent():
                nc.scalar.copy(out=lat4[:, 2 * pair:2 * pair + 2, :], in_=acc[:].rearrange("p (t n) -> p t n", t=2))
                if pair == 1:
                    deferred.append(interleave_latent)
            deferred.append(round_latent)

        def unit_kv(b):
            while len(deferred) > 0:
                flush()
            latc, lats = latent[b]
            acc = psa.tile([P, 512], F32, name="acc")
            for a1 in range(2):
                for big_g in range(2):
                    nc.tensor.matmul_mx(
                        out=acc[:, 256 * a1:256 * (a1 + 1)],
                        lhsT=latc[:, big_g, P * a1:P * (a1 + 1)].bitcast(FP8X4), lhsT_scale=lats[:, big_g, P * a1:P * (a1 + 1)],
                        rhs=up_codes[:, big_g, :].bitcast(FP8X4), rhs_scale=up_scales[:, big_g, :],
                        start=(big_g == 0), stop=(big_g == 1),
                    )
            parts = acc[:].rearrange("p (a s e j) -> p a s e j", a=2, s=2, e=2)
            prk = kvp.tile([P, 2, 2, 2, 64], F32, name="prk")
            for e1 in range(2):
                factors = trig[:, 1 - e1:3 - e1, 2 * b:2 * b + 2, :].rearrange("p e a j -> p a e j")
                nc.vector.tensor_tensor(out=prk[:, e1, :, :, :], in0=parts[:, :, 0, :, :], in1=factors, op=MULT)
            ok = kvp.tile([P, 2, 2, 64], F32, name="ok")
            vst = kvp.tile([P, 2, HEAD], F32, name="vst")
            nc.vector.tensor_copy(out=vst[:], in_=acc[:].rearrange("p (a s d) -> p a s d", a=2, s=2)[:, :, 1, :])
            nc.vector.tensor_tensor(out=ok[:], in0=prk[:, :, :, 0, :], in1=prk[:, :, :, 1, :], op=ADD)
            flush()

            def interleave_and_store():
                kst = kvp.tile([P, 2, HEAD], F32, name="kst")
                nc.scalar.copy(out=kst[:].rearrange("p a (j e) -> p a j e", e=2), in_=ok[:].rearrange("p e a j -> p a j e"))
                nc.sync.dma_start(out=k_view[:, 2 * b:2 * b + 2, :], in_=kst[:])
                nc.sync.dma_start(out=v_view[:, 2 * b:2 * b + 2, :], in_=vst[:])
            deferred.append(interleave_and_store)

        def last_job_read(unit):
            kind, b, i1, i2 = unit
            if kind == "Q":
                return max(job_index[("x", b, i1)], job_index[("wq", i2, 3)])
            if kind == "L":
                return max(job_index[("x", b, 1)], job_index[("down", i1, 2 * i2 + 1)])
            return job_index[("up", 1, 0)]

        units = []
        for big_g in range(2):
            for b in range(HEAD_BLOCKS):
                units.append(("L", b, big_g, 0))
                units.append(("L", b, big_g, 1))
        for c in range(4):
            for b in range(HEAD_BLOCKS):
                units.append(("Q", b, 0, c))
                units.append(("Q", b, 1, c))
        units.sort(key=last_job_read)
        first = units.index(("Q", 0, 0, 1))
        for b in range(HEAD_BLOCKS):
            units.insert(first + 3 * b + 2, ("KV", b, 0, 0))
        for c in range(4):
            units.append(("Q", HEAD_BLOCKS, 0, c))
        for s in range(4):
            units.append(("L", HEAD_BLOCKS, s // 2, s % 2))
        for c in range(4):
            units.append(("Q", HEAD_BLOCKS, 1, c))
        for b in range(HEAD_BLOCKS + 1, BLOCKS - 1):
            for s in range(4):
                units.append(("L", b, s // 2, s % 2))
                units.append(("Q", b, s // 2, 2 * (s % 2)))
                units.append(("Q", b, s // 2, 2 * (s % 2) + 1))
                if s == 0:
                    units.append(("KV", b - 1, 0, 0))
        b = BLOCKS - 1
        for s in range(4):
            units.append(("L", b, s // 2, s % 2))
        units.append(("KV", b - 1, 0, 0))
        for s in range(8):
            units.append(("Q", b, s // 4, s % 4))
            if s == 3:
                units.append(("KV", b, 0, 0))
        n_units = len(units)

        last_unit = {}
        for i, unit in enumerate(units):
            if unit[0] != "KV":
                last_unit[unit[1]] = i

        def units_before(job):
            if job[0] == "x" and job[1] >= X_BUFFERS:
                return last_unit[job[1] - X_BUFFERS] + 1
            return 0

        for i in range(LOADS_AHEAD):
            load(i)
        sort(0, 0)
        sort(0, 1)
        steps = []
        jobs_begun, units_done = 0, 0
        while jobs_begun < n_jobs or units_done < n_units or len(steps) > 0:
            moved = False
            wrote_unit = False
            if len(steps) == 0 and jobs_begun < n_jobs and units_before(jobs[jobs_begun]) <= units_done:
                steps.extend(job_steps(jobs_begun))
                jobs_begun += 1
            between_jobs = len(steps) == 0
            jobs_done = jobs_begun if between_jobs else jobs_begun - 1
            if units_done < n_units and last_job_read(units[units_done]) + (0 if between_jobs else JOB_LAG) < jobs_done:
                kind, b, i1, i2 = units[units_done]
                if kind == "Q":
                    unit_q(b, i1, i2)
                elif kind == "L":
                    unit_latent(b, i1, i2)
                else:
                    unit_kv(b)
                units_done += 1
                moved = True
                wrote_unit = True
            n = STEPS_PER_UNIT if jobs_begun > last_weight_job + 3 else STEPS_PER_UNIT_HEAD
            while n > 0 and len(steps) > 0:
                steps.pop(0)()
                n -= 1
                moved = True
            if not wrote_unit:
                flush()
            assert moved or len(deferred) > 0 or units_done < n_units
        while len(deferred) > 0:
            flush()
